import numpy as np
import ml_dtypes


def mxq(x, axis, fmt="e4m3"):
    dtype, down = {"e4m3": (ml_dtypes.float8_e4m3fn, 7), "e5m2": (ml_dtypes.float8_e5m2, 14)}[fmt]
    v = np.moveaxis(np.asarray(x, np.float32).astype(ml_dtypes.bfloat16).astype(np.float64), axis, -1)
    blocks = v.reshape(v.shape[:-1] + (-1, 32))
    amax = np.abs(blocks).max(-1, keepdims=True)
    byte = np.maximum(np.where(amax > 0, np.frexp(amax)[1] - 1 + 127, 0) - down, 1)
    scale = np.exp2(byte - 127.0)
    codes = (blocks / scale).astype(np.float32).astype(dtype).astype(np.float64)
    return np.moveaxis((codes * scale).reshape(v.shape), -1, axis)


WIDE = False


def mx_kscale(k):
    if not WIDE:
        return np.ones(k)
    levels = np.array([10, -10, 5, -5, 0])
    a = np.random.permutation(np.resize(levels, k // 512 * 4)).reshape(k // 512, 4)
    idx = np.arange(k)
    return np.exp2(a[idx // 512, idx % 128 // 32])


BF16 = ml_dtypes.bfloat16


def bf(x):
    return np.asarray(x, np.float32).astype(BF16)


def f64(x):
    return np.asarray(x).astype(np.float64)


B, N, DIM, H, D, M = 2, 512, 1024, 16, 64, 16
HD = H * D
HALF = D // 2
EPS = 1e-12


def l2norm(t):
    n = np.sqrt((t * t).sum(-1, keepdims=True))
    return t / np.maximum(n, EPS)


def rope(t, fr):
    rot = np.concatenate([-t[..., HALF:], t[..., :HALF]], axis=-1)
    return t * np.cos(fr) + rot * np.sin(fr)


def heads(t):
    return t.reshape(B, N, H, D).transpose(0, 2, 1, 3)


def setup_inputs():
    s = mx_kscale(DIM)
    ang = np.random.uniform(-np.pi, np.pi, (N, HALF))
    return {"x": bf(np.random.standard_normal((B, N, DIM)) * s),
            "freqs": bf(np.concatenate([ang, ang], axis=-1)),
            "Wq": bf(np.random.standard_normal((DIM, HD)) / np.sqrt(DIM) / s[:, None]),
            "Wk": bf(np.random.standard_normal((DIM, HD)) / np.sqrt(DIM) / s[:, None]),
            "Wv": bf(np.random.standard_normal((DIM, HD)) / np.sqrt(DIM) / s[:, None]),
            "mem_k": bf(np.random.standard_normal((H, M, D))),
            "mem_v": bf(np.random.standard_normal((H, M, D)))}


def reference(x, freqs, Wq, Wk, Wv, mem_k, mem_v):
    xq = mxq(f64(x), 2, "e4m3")
    fr = f64(freqs)
    q = heads(xq @ mxq(f64(Wq), 0, "e4m3"))
    k = heads(xq @ mxq(f64(Wk), 0, "e4m3"))
    v = heads(xq @ mxq(f64(Wv), 0, "e4m3"))
    q = rope(l2norm(q), fr)
    k = rope(l2norm(k), fr)
    v = rope(v, fr)
    mk = np.broadcast_to(l2norm(f64(mem_k))[None], (B, H, M, D))
    mv = np.broadcast_to(f64(mem_v)[None], (B, H, M, D))
    return q, np.concatenate([mk, k], axis=2), np.concatenate([mv, v], axis=2)

@@ -1,0 +1,224 @@
+from contextlib import ExitStack
+
+import concourse.mybir as mybir
+from concourse.masks import make_identity
+
+F32 = mybir.dt.float32
+BF16 = mybir.dt.bfloat16
+U32 = mybir.dt.uint32
+U8 = mybir.dt.uint8
+FP8X4 = mybir.dt.float8_e4m3fn_x4
+ACT = mybir.ActivationFunctionType
+ALU = mybir.AluOpType
+
+BATCH, POSITIONS, DIM, HEADS, FEATURES, MEM_SLOTS = 2, 512, 1024, 16, 64, 16
+HALF = FEATURES // 2
+EPS = 1e-12
+
+P = 128
+PACK = 4
+K_PASS = P * PACK
+PASSES = DIM // K_PASS
+TILES_PER_BATCH = POSITIONS // P
+TOKEN_TILES = BATCH * TILES_PER_BATCH
+BANK_COLUMNS = 512
+BANK_HEADS = BANK_COLUMNS // FEATURES
+RANGES_PER_WEIGHT = HEADS // BANK_HEADS
+WORDS_PER_TOKEN = DIM // 2
+
+FLOPS = 2 * BATCH * POSITIONS * DIM * 3 * HEADS * FEATURES
+
+
+def tile_attention_pa_kernel(tc, x, freqs, Wq, Wk, Wv, mem_k, mem_v, out_q, out_k, out_v):
+    nc = tc.nc
+    weights = [Wq, Wk, Wv]
+    outputs = [out_q, out_k, out_v]
+    first_position = [0, MEM_SLOTS, MEM_SLOTS]
+    normalised = [True, True, False]
+    ranges = len(weights) * RANGES_PER_WEIGHT
+
+    with ExitStack() as ctx:
+        keep = ctx.enter_context(tc.tile_pool(name="keep", bufs=1))
+        stage = ctx.enter_context(tc.tile_pool(name="stage", bufs=2))
+        norms = ctx.enter_context(tc.tile_pool(name="norms", bufs=4))
+        rotated = ctx.enter_context(tc.tile_pool(name="rotated", bufs=4))
+        results = ctx.enter_context(tc.tile_pool(name="results", bufs=3))
+        psum_x = ctx.enter_context(tc.psum_pool(name="psum_x", bufs=2))
+        psum_acc = ctx.enter_context(tc.psum_pool(name="psum_acc", bufs=6))
+
+        x_raw = [keep.tile([P, TILES_PER_BATCH * DIM], BF16, name="x_raw%d" % b) for b in range(BATCH)]
+        w_raw = [
+            [keep.tile([P, PACK * HEADS * FEATURES], BF16, name="w_raw%d_%d" % (w, g)) for g in range(PASSES)]
+            for w in range(len(weights))
+        ]
+
+        def load_x(b):
+            nc.sync.dma_start(out=x_raw[b][:], in_=x[b].rearrange("(p j) k -> p (j k)", j=TILES_PER_BATCH))
+
+        def load_w(w):
+            for g in range(PASSES):
+                nc.sync.dma_start(
+                    out=w_raw[w][g][:].rearrange("p (u m) -> p u m", u=2),
+                    in_=weights[w][g * K_PASS : (g + 1) * K_PASS, :].rearrange("(u p e) n -> p u (e n)", u=2, e=2),
+                )
+
+        load_x(0)
+        load_w(0)
+        load_x(1)
+        load_w(1)
+        load_w(2)
+
+        angles = keep.tile([P, TILES_PER_BATCH, 2, HALF], BF16)
+        nc.scalar.dma_start(out=angles[:], in_=freqs.rearrange("(p j) (a c) -> p j a c", j=TILES_PER_BATCH, a=2))
+        mem_k_raw = keep.tile([HEADS, MEM_SLOTS, FEATURES], BF16)
+        nc.scalar.dma_start(out=mem_k_raw[:], in_=mem_k)
+        mem_v_raw = keep.tile([HEADS, MEM_SLOTS, FEATURES], BF16)
+        nc.scalar.dma_start(out=mem_v_raw[:], in_=mem_v)
+
+        identity = keep.tile([P, P], F32)
+        make_identity(nc, identity[:])
+
+        table = keep.tile([P, TILES_PER_BATCH, 2, 2, HALF], F32)
+        nc.scalar.activation(out=table[:, :, 0, 1, :], in_=angles[:, :, 1, :], func=ACT.Sin)
+        nc.scalar.activation(out=table[:, :, 1, 0, :], in_=angles[:, :, 0, :], func=ACT.Sin, scale=-1.0)
+        half_sin = keep.tile([P, TILES_PER_BATCH, 2, HALF], F32)
+        nc.scalar.activation(out=half_sin[:], in_=angles[:], func=ACT.Sin, scale=0.5)
+        half_sin_sq = keep.tile([P, TILES_PER_BATCH, 2, HALF], F32)
+        nc.vector.tensor_tensor(out=half_sin_sq[:], in0=half_sin[:], in1=half_sin[:], op=ALU.mult)
+        for a in range(2):
+            nc.vector.tensor_scalar(
+                out=table[:, :, a, a, :], in0=half_sin_sq[:, :, a, :], scalar1=-2.0, scalar2=1.0, op0=ALU.mult, op1=ALU.add
+            )
+
+        mem_k_sq = keep.tile([HEADS, MEM_SLOTS, FEATURES], F32)
+        nc.scalar.activation(out=mem_k_sq[:], in_=mem_k_raw[:], func=ACT.Square)
+        mem_k_ss = keep.tile([HEADS, MEM_SLOTS], F32)
+        nc.vector.tensor_reduce(out=mem_k_ss[:], in_=mem_k_sq[:], axis=mybir.AxisListType.X, op=ALU.add)
+        mem_k_rsqrt = keep.tile([HEADS, MEM_SLOTS], F32)
+        nc.scalar.activation(out=mem_k_rsqrt[:], in_=mem_k_ss[:], func=ACT.Abs_reciprocal_sqrt)
+        mem_k_factor = keep.tile([HEADS, MEM_SLOTS], F32)
+        nc.vector.tensor_scalar_min(out=mem_k_factor[:], in0=mem_k_rsqrt[:], scalar1=1.0 / EPS)
+        mem_k_out = keep.tile([HEADS, MEM_SLOTS, FEATURES], F32)
+        nc.vector.tensor_tensor(
+            out=mem_k_out[:],
+            in0=mem_k_raw[:],
+            in1=mem_k_factor[:].unsqueeze(2).to_broadcast([HEADS, MEM_SLOTS, FEATURES]),
+            op=ALU.mult,
+        )
+        mem_v_out = keep.tile([HEADS, MEM_SLOTS, FEATURES], F32)
+        nc.vector.tensor_copy(out=mem_v_out[:], in_=mem_v_raw[:])
+        for b in range(BATCH):
+            nc.scalar.dma_start(out=out_k[b, :, 0:MEM_SLOTS, :], in_=mem_k_out[:])
+            nc.scalar.dma_start(out=out_v[b, :, 0:MEM_SLOTS, :], in_=mem_v_out[:])
+
+        x_codes = keep.tile([P, TOKEN_TILES, PASSES * P], U32, align_bytes=64)
+        x_scales = keep.tile([P, TOKEN_TILES, PASSES * P], U8, align_bytes=64)
+        w_codes = keep.tile([P, ranges, PASSES * BANK_COLUMNS], U32, align_bytes=64)
+        w_scales = keep.tile([P, ranges, PASSES * BANK_COLUMNS], U8, align_bytes=64)
+
+        def quantise_x_tile(b, j):
+            words = x_raw[b][:].bitcast(F32)
+            transposed = psum_x.tile([P, PASSES * 2, P], F32)
+            for gu in range(PASSES * 2):
+                first_word = j * WORDS_PER_TOKEN + gu * P
+                nc.tensor.transpose(transposed[:, gu, :], words[:, first_word : first_word + P], identity[:])
+            x_grouped = stage.tile([P, PASSES * P * PACK], BF16, align_bytes=64)
+            nc.scalar.copy(
+                out=x_grouped[:].bitcast(F32).rearrange("p (g r u) -> p g r u", g=PASSES, u=2),
+                in_=transposed[:].rearrange("p (g u) r -> p g r u", g=PASSES),
+            )
+            token_tile = b * TILES_PER_BATCH + j
+            nc.vector.quantize_mx(
+                out=x_codes[:, token_tile, :].bitcast(FP8X4), scales=x_scales[:, token_tile, :], in_=x_grouped[:]
+            )
+
+        def quantise_w_range(r):
+            w, part = divmod(r, RANGES_PER_WEIGHT)
+            w_grouped = stage.tile([P, PASSES, BANK_COLUMNS, PACK], BF16, align_bytes=64)
+            for g in range(PASSES):
+                rows = w_raw[w][g][:].rearrange("p (t n) -> p t n", t=PACK)
+                rows = rows[:, :, part * BANK_COLUMNS : (part + 1) * BANK_COLUMNS]
+                source = rows.rearrange("p t (c i) -> p c t i", i=4)
+                target = w_grouped[:, g].rearrange("p (c i) t -> p c t i", i=4)
+                if g == 0:
+                    nc.vector.tensor_copy(out=target, in_=source)
+                else:
+                    nc.scalar.copy(out=target, in_=source)
+            nc.vector.quantize_mx(
+                out=w_codes[:, r, :].bitcast(FP8X4),
+                scales=w_scales[:, r, :],
+                in_=w_grouped[:].rearrange("p g n t -> p (g n t)"),
+            )
+
+        def project_and_rotate(r, b, j, result):
+            token_tile = b * TILES_PER_BATCH + j
+            acc = psum_acc.tile([P, BANK_COLUMNS], F32)
+            for g in range(PASSES):
+                tokens = slice(g * P, (g + 1) * P)
+                columns = slice(g * BANK_COLUMNS, (g + 1) * BANK_COLUMNS)
+                nc.tensor.matmul_mx(
+                    out=acc[:],
+                    lhsT=x_codes[:, token_tile, tokens].bitcast(FP8X4),
+                    lhsT_scale=x_scales[:, token_tile, tokens],
+                    rhs=w_codes[:, r, columns].bitcast(FP8X4),
+                    rhs_scale=w_scales[:, r, columns],
+                    start=(g == 0),
+                    stop=(g == PASSES - 1),
+                )
+            scaled = normalised[r // RANGES_PER_WEIGHT]
+            if scaled:
+                squares = stage.tile([P, BANK_HEADS, FEATURES], F32)
+                sum_sq = norms.tile([P, BANK_HEADS], F32)
+                for h in range(BANK_HEADS):
+                    nc.scalar.activation(
+                        out=squares[:, h, :],
+                        in_=acc[:, h * FEATURES : (h + 1) * FEATURES],
+                        func=ACT.Square,
+                        accum_out=sum_sq[:, h : h + 1],
+                    )
+                rsqrt = norms.tile([P, BANK_HEADS], F32)
+                nc.scalar.activation(out=rsqrt[:], in_=sum_sq[:], func=ACT.Abs_reciprocal_sqrt)
+                factor = norms.tile([P, BANK_HEADS], F32)
+                nc.vector.tensor_scalar_min(out=factor[:], in0=rsqrt[:], scalar1=1.0 / EPS)
+            shape = [P, BANK_HEADS, 2, 2, HALF]
+            products = rotated.tile(shape, F32)
+            nc.vector.tensor_tensor(
+                out=products[:],
+                in0=acc[:].rearrange("p (h a c) -> p h a c", a=2, c=HALF).unsqueeze(3).to_broadcast(shape),
+                in1=table[:, j].unsqueeze(1).to_broadcast(shape),
+                op=ALU.mult,
+            )
+            nc.gpsimd.tensor_tensor(
+                out=result[:, :, j, :],
+                in0=products[:, :, 0].rearrange("p h o c -> p h (o c)"),
+                in1=products[:, :, 1].rearrange("p h o c -> p h (o c)"),
+                op=ALU.add,
+            )
+            if scaled:
+                for h in range(BANK_HEADS):
+                    nc.scalar.activation(
+                        out=result[:, h, j, :], in_=result[:, h, j, :], func=ACT.Copy, scale=factor[:, h : h + 1]
+                    )
+
+        def store(r, b, result):
+            w, part = divmod(r, RANGES_PER_WEIGHT)
+            heads = slice(part * BANK_HEADS, (part + 1) * BANK_HEADS)
+            positions = slice(first_position[w], first_position[w] + POSITIONS)
+            nc.sync.dma_start(
+                out=outputs[w][b, heads, positions, :].rearrange("h (p j) d -> p h (j d)", j=TILES_PER_BATCH),
+                in_=result[:].rearrange("p h j d -> p h (j d)"),
+            )
+
+        for j in range(TILES_PER_BATCH):
+            quantise_x_tile(0, j)
+        quantise_w_range(0)
+        for j in range(TILES_PER_BATCH):
+            quantise_x_tile(1, j)
+        for r in range(ranges):
+            if r + 1 < ranges:
+                quantise_w_range(r + 1)
+            for b in range(BATCH):
+                result = results.tile([P, BANK_HEADS, TILES_PER_BATCH, FEATURES], F32)
+                for j in range(TILES_PER_BATCH):
+                    project_and_rotate(r, b, j, result)
+                store(r, b, result)

@@ -19,12 +19,15 @@ P = 128
 PACK = 4
 K_PASS = P * PACK
 PASSES = DIM // K_PASS
+VECTOR_PASS, SCALAR_PASS = 0, 1
 TILES_PER_BATCH = POSITIONS // P
 TOKEN_TILES = BATCH * TILES_PER_BATCH
+TILES_PER_STORE = 2
 BANK_COLUMNS = 512
 BANK_HEADS = BANK_COLUMNS // FEATURES
-RANGES_PER_WEIGHT = HEADS // BANK_HEADS
-WORDS_PER_TOKEN = DIM // 2
+PARTS = HEADS // BANK_HEADS
+UNITS = PARTS * TOKEN_TILES
+WORDS_PER_PASS = K_PASS // 2
 
 FLOPS = 2 * BATCH * POSITIONS * DIM * 3 * HEADS * FEATURES
 
@@ -35,7 +38,12 @@ def tile_attention_pa_kernel(tc, x, freqs, Wq, Wk, Wv, mem_k, mem_v, out_q, out_
     outputs = [out_q, out_k, out_v]
     first_position = [0, MEM_SLOTS, MEM_SLOTS]
     normalised = [True, True, False]
-    ranges = len(weights) * RANGES_PER_WEIGHT
+
+    banks = []
+    for step in range(UNITS + len(weights) - 1):
+        for w in range(len(weights)):
+            if 0 <= step - w < UNITS:
+                banks.append((w, step - w))
 
     with ExitStack() as ctx:
         keep = ctx.enter_context(tc.tile_pool(name="keep", bufs=1))
@@ -46,34 +54,33 @@ def tile_attention_pa_kernel(tc, x, freqs, Wq, Wk, Wv, mem_k, mem_v, out_q, out_
         psum_x = ctx.enter_context(tc.psum_pool(name="psum_x", bufs=2))
         psum_acc = ctx.enter_context(tc.psum_pool(name="psum_acc", bufs=6))
 
-        x_raw = [keep.tile([P, TILES_PER_BATCH * DIM], BF16, name="x_raw%d" % b) for b in range(BATCH)]
-        w_raw = [
-            [keep.tile([P, PACK * HEADS * FEATURES], BF16, name="w_raw%d_%d" % (w, g)) for g in range(PASSES)]
-            for w in range(len(weights))
-        ]
-
-        def load_x(b):
-            nc.sync.dma_start(out=x_raw[b][:], in_=x[b].rearrange("(p j) k -> p (j k)", j=TILES_PER_BATCH))
-
-        def load_w(w):
-            for g in range(PASSES):
-                nc.sync.dma_start(
-                    out=w_raw[w][g][:].rearrange("p (u m) -> p u m", u=2),
-                    in_=weights[w][g * K_PASS : (g + 1) * K_PASS, :].rearrange("(u p e) n -> p u (e n)", u=2, e=2),
-                )
-
-        load_x(0)
-        load_w(0)
-        load_x(1)
-        load_w(1)
-        load_w(2)
-
         angles = keep.tile([P, TILES_PER_BATCH, 2, HALF], BF16)
         nc.scalar.dma_start(out=angles[:], in_=freqs.rearrange("(p j) (a c) -> p j a c", j=TILES_PER_BATCH, a=2))
         mem_k_raw = keep.tile([HEADS, MEM_SLOTS, FEATURES], BF16)
         nc.scalar.dma_start(out=mem_k_raw[:], in_=mem_k)
         mem_v_raw = keep.tile([HEADS, MEM_SLOTS, FEATURES], BF16)
         nc.scalar.dma_start(out=mem_v_raw[:], in_=mem_v)
+
+        x_raw = [keep.tile([P, DIM], BF16, name="x_raw%d" % t) for t in range(TOKEN_TILES)]
+        w_raw = [
+            [keep.tile([P, PASSES, PACK, BANK_COLUMNS], BF16, name="w_raw%d_%d" % (w, part)) for part in range(PARTS)]
+            for w in range(len(weights))
+        ]
+        for w, unit in banks:
+            part, token_tile = divmod(unit, TOKEN_TILES)
+            if w == 0 and part == 0:
+                b, j = divmod(token_tile, TILES_PER_BATCH)
+                nc.sync.dma_start(
+                    out=x_raw[token_tile][:], in_=x[b].rearrange("(p j) k -> p j k", j=TILES_PER_BATCH)[:, j, :]
+                )
+            if token_tile == 0:
+                for g in (SCALAR_PASS, VECTOR_PASS):
+                    nc.sync.dma_start(
+                        out=w_raw[w][part][:, g],
+                        in_=weights[w][
+                            g * K_PASS : (g + 1) * K_PASS, part * BANK_COLUMNS : (part + 1) * BANK_COLUMNS
+                        ].rearrange("(p t) n -> p t n", t=PACK),
+                    )
 
         identity = keep.tile([P, P], F32)
         make_identity(nc, identity[:])
@@ -99,48 +106,50 @@ def tile_attention_pa_kernel(tc, x, freqs, Wq, Wk, Wv, mem_k, mem_v, out_q, out_
         mem_k_factor = keep.tile([HEADS, MEM_SLOTS], F32)
         nc.vector.tensor_scalar_min(out=mem_k_factor[:], in0=mem_k_rsqrt[:], scalar1=1.0 / EPS)
         mem_k_out = keep.tile([HEADS, MEM_SLOTS, FEATURES], F32)
-        nc.vector.tensor_tensor(
+        nc.gpsimd.tensor_tensor(
             out=mem_k_out[:],
             in0=mem_k_raw[:],
             in1=mem_k_factor[:].unsqueeze(2).to_broadcast([HEADS, MEM_SLOTS, FEATURES]),
             op=ALU.mult,
         )
         mem_v_out = keep.tile([HEADS, MEM_SLOTS, FEATURES], F32)
-        nc.vector.tensor_copy(out=mem_v_out[:], in_=mem_v_raw[:])
+        nc.gpsimd.tensor_scalar(
+            out=mem_v_out[:], in0=mem_v_raw[:], scalar1=1.0, scalar2=0.0, op0=ALU.mult, op1=ALU.add
+        )
         for b in range(BATCH):
             nc.scalar.dma_start(out=out_k[b, :, 0:MEM_SLOTS, :], in_=mem_k_out[:])
             nc.scalar.dma_start(out=out_v[b, :, 0:MEM_SLOTS, :], in_=mem_v_out[:])
 
         x_codes = keep.tile([P, TOKEN_TILES, PASSES * P], U32, align_bytes=64)
         x_scales = keep.tile([P, TOKEN_TILES, PASSES * P], U8, align_bytes=64)
-        w_codes = keep.tile([P, ranges, PASSES * BANK_COLUMNS], U32, align_bytes=64)
-        w_scales = keep.tile([P, ranges, PASSES * BANK_COLUMNS], U8, align_bytes=64)
+        w_codes = keep.tile([P, len(weights) * PARTS, PASSES * BANK_COLUMNS], U32, align_bytes=64)
+        w_scales = keep.tile([P, len(weights) * PARTS, PASSES * BANK_COLUMNS], U8, align_bytes=64)
 
-        def quantise_x_tile(b, j):
-            words = x_raw[b][:].bitcast(F32)
+        def quantise_x_tile(token_tile):
+            words = x_raw[token_tile][:].bitcast(F32)
             transposed = psum_x.tile([P, PASSES * 2, P], F32)
-            for gu in range(PASSES * 2):
-                first_word = j * WORDS_PER_TOKEN + gu * P
-                nc.tensor.transpose(transposed[:, gu, :], words[:, first_word : first_word + P], identity[:])
+            for g in range(PASSES):
+                for u in range(2):
+                    first_word = g * WORDS_PER_PASS + u
+                    nc.tensor.transpose(
+                        transposed[:, 2 * g + u, :], words[:, first_word : first_word + WORDS_PER_PASS - 1 : 2], identity[:]
+                    )
             x_grouped = stage.tile([P, PASSES * P * PACK], BF16, align_bytes=64)
             nc.scalar.copy(
                 out=x_grouped[:].bitcast(F32).rearrange("p (g r u) -> p g r u", g=PASSES, u=2),
                 in_=transposed[:].rearrange("p (g u) r -> p g r u", g=PASSES),
             )
-            token_tile = b * TILES_PER_BATCH + j
             nc.vector.quantize_mx(
                 out=x_codes[:, token_tile, :].bitcast(FP8X4), scales=x_scales[:, token_tile, :], in_=x_grouped[:]
             )
 
-        def quantise_w_range(r):
-            w, part = divmod(r, RANGES_PER_WEIGHT)
+        def quantise_w_range(w, part):
+            r = w * PARTS + part
             w_grouped = stage.tile([P, PASSES, BANK_COLUMNS, PACK], BF16, align_bytes=64)
-            for g in range(PASSES):
-                rows = w_raw[w][g][:].rearrange("p (t n) -> p t n", t=PACK)
-                rows = rows[:, :, part * BANK_COLUMNS : (part + 1) * BANK_COLUMNS]
-                source = rows.rearrange("p t (c i) -> p c t i", i=4)
+            for g in (SCALAR_PASS, VECTOR_PASS):
+                source = w_raw[w][part][:, g].rearrange("p t (c i) -> p c t i", i=4)
                 target = w_grouped[:, g].rearrange("p (c i) t -> p c t i", i=4)
-                if g == 0:
+                if g == VECTOR_PASS:
                     nc.vector.tensor_copy(out=target, in_=source)
                 else:
                     nc.scalar.copy(out=target, in_=source)
@@ -150,8 +159,8 @@ def tile_attention_pa_kernel(tc, x, freqs, Wq, Wk, Wv, mem_k, mem_v, out_q, out_
                 in_=w_grouped[:].rearrange("p g n t -> p (g n t)"),
             )
 
-        def project_and_rotate(r, b, j, result):
-            token_tile = b * TILES_PER_BATCH + j
+        def project_and_rotate(w, part, token_tile, rows):
+            r = w * PARTS + part
             acc = psum_acc.tile([P, BANK_COLUMNS], F32)
             for g in range(PASSES):
                 tokens = slice(g * P, (g + 1) * P)
@@ -165,8 +174,7 @@ def tile_attention_pa_kernel(tc, x, freqs, Wq, Wk, Wv, mem_k, mem_v, out_q, out_
                     start=(g == 0),
                     stop=(g == PASSES - 1),
                 )
-            scaled = normalised[r // RANGES_PER_WEIGHT]
-            if scaled:
+            if normalised[w]:
                 squares = stage.tile([P, BANK_HEADS, FEATURES], F32)
                 sum_sq = norms.tile([P, BANK_HEADS], F32)
                 for h in range(BANK_HEADS):
@@ -185,40 +193,36 @@ def tile_attention_pa_kernel(tc, x, freqs, Wq, Wk, Wv, mem_k, mem_v, out_q, out_
             nc.vector.tensor_tensor(
                 out=products[:],
                 in0=acc[:].rearrange("p (h a c) -> p h a c", a=2, c=HALF).unsqueeze(3).to_broadcast(shape),
-                in1=table[:, j].unsqueeze(1).to_broadcast(shape),
+                in1=table[:, token_tile % TILES_PER_BATCH].unsqueeze(1).to_broadcast(shape),
                 op=ALU.mult,
             )
             nc.gpsimd.tensor_tensor(
-                out=result[:, :, j, :],
+                out=rows,
                 in0=products[:, :, 0].rearrange("p h o c -> p h (o c)"),
                 in1=products[:, :, 1].rearrange("p h o c -> p h (o c)"),
                 op=ALU.add,
             )
-            if scaled:
+            if normalised[w]:
                 for h in range(BANK_HEADS):
-                    nc.scalar.activation(
-                        out=result[:, h, j, :], in_=result[:, h, j, :], func=ACT.Copy, scale=factor[:, h : h + 1]
-                    )
+                    nc.scalar.activation(out=rows[:, h, :], in_=rows[:, h, :], func=ACT.Copy, scale=factor[:, h : h + 1])
 
-        def store(r, b, result):
-            w, part = divmod(r, RANGES_PER_WEIGHT)
+        def store(w, part, b, first_tile, result):
             heads = slice(part * BANK_HEADS, (part + 1) * BANK_HEADS)
             positions = slice(first_position[w], first_position[w] + POSITIONS)
-            nc.sync.dma_start(
-                out=outputs[w][b, heads, positions, :].rearrange("h (p j) d -> p h (j d)", j=TILES_PER_BATCH),
-                in_=result[:].rearrange("p h j d -> p h (j d)"),
-            )
+            by_tile = outputs[w][b, heads, positions, :].rearrange("h (p j) d -> p h j d", j=TILES_PER_BATCH)
+            nc.sync.dma_start(out=by_tile[:, :, first_tile : first_tile + TILES_PER_STORE, :], in_=result[:])
 
-        for j in range(TILES_PER_BATCH):
-            quantise_x_tile(0, j)
-        quantise_w_range(0)
-        for j in range(TILES_PER_BATCH):
-            quantise_x_tile(1, j)
-        for r in range(ranges):
-            if r + 1 < ranges:
-                quantise_w_range(r + 1)
-            for b in range(BATCH):
-                result = results.tile([P, BANK_HEADS, TILES_PER_BATCH, FEATURES], F32)
-                for j in range(TILES_PER_BATCH):
-                    project_and_rotate(r, b, j, result)
-                store(r, b, result)
+        open_result = [None] * len(weights)
+        for w, unit in banks:
+            part, token_tile = divmod(unit, TOKEN_TILES)
+            b, j = divmod(token_tile, TILES_PER_BATCH)
+            place = j % TILES_PER_STORE
+            if w == 0 and part == 0:
+                quantise_x_tile(token_tile)
+            if token_tile == 0:
+                quantise_w_range(w, part)
+            if place == 0:
+                open_result[w] = results.tile([P, BANK_HEADS, TILES_PER_STORE, FEATURES], F32, name="result%d" % w)
+            project_and_rotate(w, part, token_tile, open_result[w][:, :, place, :])
+            if place == TILES_PER_STORE - 1:
+                store(w, part, b, j - place, open_result[w])

@@ -212,15 +212,18 @@ def tile_attention_pa_kernel(tc, x, freqs, Wq, Wk, Wv, mem_k, mem_v, out_q, out_
             by_tile = outputs[w][b, heads, positions, :].rearrange("h (p j) d -> p h j d", j=TILES_PER_BATCH)
             nc.sync.dma_start(out=by_tile[:, :, first_tile : first_tile + TILES_PER_STORE, :], in_=result[:])
 
+        for w, unit in banks:
+            part, token_tile = divmod(unit, TOKEN_TILES)
+            if w == 0 and part == 0:
+                quantise_x_tile(token_tile)
+            if token_tile == 0:
+                quantise_w_range(w, part)
+
         open_result = [None] * len(weights)
         for w, unit in banks:
             part, token_tile = divmod(unit, TOKEN_TILES)
             b, j = divmod(token_tile, TILES_PER_BATCH)
             place = j % TILES_PER_STORE
-            if w == 0 and part == 0:
-                quantise_x_tile(token_tile)
-            if token_tile == 0:
-                quantise_w_range(w, part)
             if place == 0:
                 open_result[w] = results.tile([P, BANK_HEADS, TILES_PER_STORE, FEATURES], F32, name="result%d" % w)
             project_and_rotate(w, part, token_tile, open_result[w][:, :, place, :])

@@ -86,8 +86,8 @@ def tile_attention_pa_kernel(tc, x, freqs, Wq, Wk, Wv, mem_k, mem_v, out_q, out_
         make_identity(nc, identity[:])
 
         table = keep.tile([P, TILES_PER_BATCH, 2, 2, HALF], F32)
-        nc.scalar.activation(out=table[:, :, 0, 1, :], in_=angles[:, :, 1, :], func=ACT.Sin)
-        nc.scalar.activation(out=table[:, :, 1, 0, :], in_=angles[:, :, 0, :], func=ACT.Sin, scale=-1.0)
+        nc.scalar.activation(out=table[:, :, 1, 0, :], in_=angles[:, :, 1, :], func=ACT.Sin)
+        nc.scalar.activation(out=table[:, :, 0, 1, :], in_=angles[:, :, 0, :], func=ACT.Sin, scale=-1.0)
         half_sin = keep.tile([P, TILES_PER_BATCH, 2, HALF], F32)
         nc.scalar.activation(out=half_sin[:], in_=angles[:], func=ACT.Sin, scale=0.5)
         half_sin_sq = keep.tile([P, TILES_PER_BATCH, 2, HALF], F32)
@@ -184,27 +184,38 @@ def tile_attention_pa_kernel(tc, x, freqs, Wq, Wk, Wv, mem_k, mem_v, out_q, out_
                         func=ACT.Square,
                         accum_out=sum_sq[:, h : h + 1],
                     )
-                rsqrt = norms.tile([P, BANK_HEADS], F32)
-                nc.scalar.activation(out=rsqrt[:], in_=sum_sq[:], func=ACT.Abs_reciprocal_sqrt)
+                above = norms.tile([P, BANK_HEADS], F32)
+                nc.scalar.activation(out=above[:], in_=sum_sq[:], func=ACT.Relu, bias=-EPS * EPS)
                 factor = norms.tile([P, BANK_HEADS], F32)
-                nc.vector.tensor_scalar_min(out=factor[:], in0=rsqrt[:], scalar1=1.0 / EPS)
-            shape = [P, BANK_HEADS, 2, 2, HALF]
+                nc.scalar.activation(out=factor[:], in_=above[:], func=ACT.Abs_reciprocal_sqrt, bias=EPS * EPS)
+            shape = [P, BANK_HEADS, 2, FEATURES]
             products = rotated.tile(shape, F32)
-            nc.vector.tensor_tensor(
-                out=products[:],
-                in0=acc[:].rearrange("p (h a c) -> p h a c", a=2, c=HALF).unsqueeze(3).to_broadcast(shape),
-                in1=table[:, token_tile % TILES_PER_BATCH].unsqueeze(1).to_broadcast(shape),
-                op=ALU.mult,
-            )
-            nc.gpsimd.tensor_tensor(
-                out=rows,
-                in0=products[:, :, 0].rearrange("p h o c -> p h (o c)"),
-                in1=products[:, :, 1].rearrange("p h o c -> p h (o c)"),
-                op=ALU.add,
-            )
+            spread = acc[:].rearrange("p (h d) -> p h d", d=FEATURES).unsqueeze(2).to_broadcast(shape)
+            factors_of_tile = table[:, token_tile % TILES_PER_BATCH].rearrange("p o a c -> p o (a c)")
             if normalised[w]:
                 for h in range(BANK_HEADS):
-                    nc.scalar.activation(out=rows[:, h, :], in_=rows[:, h, :], func=ACT.Copy, scale=factor[:, h : h + 1])
+                    nc.vector.scalar_tensor_tensor(
+                        out=products[:, h],
+                        in0=spread[:, h],
+                        scalar=factor[:, h : h + 1],
+                        in1=factors_of_tile,
+                        op0=ALU.mult,
+                        op1=ALU.mult,
+                    )
+            else:
+                nc.vector.tensor_tensor(
+                    out=products[:],
+                    in0=spread,
+                    in1=factors_of_tile.unsqueeze(1).to_broadcast(shape),
+                    op=ALU.mult,
+                )
+            by_half = products[:].rearrange("p h o (a c) -> p h o a c", a=2)
+            nc.gpsimd.tensor_tensor(
+                out=rows.rearrange("p h (o c) -> p h o c", o=2),
+                in0=by_half[:, :, :, 0, :],
+                in1=by_half[:, :, :, 1, :],
+                op=ALU.add,
+            )
 
         def store(w, part, b, first_tile, result):
             heads = slice(part * BANK_HEADS, (part + 1) * BANK_HEADS)

@@ -127,7 +127,7 @@ def tile_attention_pa_kernel(tc, x, freqs, Wq, Wk, Wv, mem_k, mem_v, out_q, out_
 
         def quantise_x_tile(token_tile):
             words = x_raw[token_tile][:].bitcast(F32)
-            transposed = psum_x.tile([P, PASSES * 2, P], F32)
+            transposed = psum_x.tile([P, PASSES * 2, P], F32, name="aux")
             for g in range(PASSES):
                 for u in range(2):
                     first_word = g * WORDS_PER_PASS + u
@@ -210,6 +210,12 @@ def tile_attention_pa_kernel(tc, x, freqs, Wq, Wk, Wv, mem_k, mem_v, out_q, out_
                     op=ALU.mult,
                 )
             by_half = products[:].rearrange("p h o (a c) -> p h o a c", a=2)
+            if w == 0 and token_tile % 2 == 0:
+                total = psum_x.tile([P, BANK_HEADS, 2, HALF], F32, name="aux")
+                for a in range(2):
+                    nc.tensor.matmul(out=total[:], lhsT=identity[:], rhs=by_half[:, :, :, a, :], start=(a == 0), stop=(a == 1))
+                nc.scalar.copy(out=rows.rearrange("p h (o c) -> p h o c", o=2), in_=total[:])
+                return
             nc.gpsimd.tensor_tensor(
                 out=rows.rearrange("p h (o c) -> p h o c", o=2),
                 in0=by_half[:, :, :, 0, :],

@@ -97,29 +97,6 @@ def tile_attention_pa_kernel(tc, x, freqs, Wq, Wk, Wv, mem_k, mem_v, out_q, out_
                 out=table[:, :, a, a, :], in0=half_sin_sq[:, :, a, :], scalar1=-2.0, scalar2=1.0, op0=ALU.mult, op1=ALU.add
             )
 
-        mem_k_sq = keep.tile([HEADS, MEM_SLOTS, FEATURES], F32)
-        nc.scalar.activation(out=mem_k_sq[:], in_=mem_k_raw[:], func=ACT.Square)
-        mem_k_ss = keep.tile([HEADS, MEM_SLOTS], F32)
-        nc.vector.tensor_reduce(out=mem_k_ss[:], in_=mem_k_sq[:], axis=mybir.AxisListType.X, op=ALU.add)
-        mem_k_rsqrt = keep.tile([HEADS, MEM_SLOTS], F32)
-        nc.scalar.activation(out=mem_k_rsqrt[:], in_=mem_k_ss[:], func=ACT.Abs_reciprocal_sqrt)
-        mem_k_factor = keep.tile([HEADS, MEM_SLOTS], F32)
-        nc.vector.tensor_scalar_min(out=mem_k_factor[:], in0=mem_k_rsqrt[:], scalar1=1.0 / EPS)
-        mem_k_out = keep.tile([HEADS, MEM_SLOTS, FEATURES], F32)
-        nc.gpsimd.tensor_tensor(
-            out=mem_k_out[:],
-            in0=mem_k_raw[:],
-            in1=mem_k_factor[:].unsqueeze(2).to_broadcast([HEADS, MEM_SLOTS, FEATURES]),
-            op=ALU.mult,
-        )
-        mem_v_out = keep.tile([HEADS, MEM_SLOTS, FEATURES], F32)
-        nc.gpsimd.tensor_scalar(
-            out=mem_v_out[:], in0=mem_v_raw[:], scalar1=1.0, scalar2=0.0, op0=ALU.mult, op1=ALU.add
-        )
-        for b in range(BATCH):
-            nc.scalar.dma_start(out=out_k[b, :, 0:MEM_SLOTS, :], in_=mem_k_out[:])
-            nc.scalar.dma_start(out=out_v[b, :, 0:MEM_SLOTS, :], in_=mem_v_out[:])
-
         x_codes = keep.tile([P, TOKEN_TILES, PASSES * P], U32, align_bytes=64)
         x_scales = keep.tile([P, TOKEN_TILES, PASSES * P], U8, align_bytes=64)
         w_codes = keep.tile([P, len(weights) * PARTS, PASSES * BANK_COLUMNS], U32, align_bytes=64)
@@ -192,7 +169,8 @@ def tile_attention_pa_kernel(tc, x, freqs, Wq, Wk, Wv, mem_k, mem_v, out_q, out_
             products = rotated.tile(shape, F32)
             spread = acc[:].rearrange("p (h d) -> p h d", d=FEATURES).unsqueeze(2).to_broadcast(shape)
             factors_of_tile = table[:, token_tile % TILES_PER_BATCH].rearrange("p o a c -> p o (a c)")
-            if normalised[w]:
+            added_by_tensor = w == 0 and token_tile % 2 == 0
+            if normalised[w] and not added_by_tensor:
                 for h in range(BANK_HEADS):
                     nc.vector.scalar_tensor_tensor(
                         out=products[:, h],
@@ -210,11 +188,17 @@ def tile_attention_pa_kernel(tc, x, freqs, Wq, Wk, Wv, mem_k, mem_v, out_q, out_
                     op=ALU.mult,
                 )
             by_half = products[:].rearrange("p h o (a c) -> p h o a c", a=2)
-            if w == 0 and token_tile % 2 == 0:
+            if added_by_tensor:
                 total = psum_x.tile([P, BANK_HEADS, 2, HALF], F32, name="aux")
                 for a in range(2):
                     nc.tensor.matmul(out=total[:], lhsT=identity[:], rhs=by_half[:, :, :, a, :], start=(a == 0), stop=(a == 1))
-                nc.scalar.copy(out=rows.rearrange("p h (o c) -> p h o c", o=2), in_=total[:])
+                for h in range(BANK_HEADS):
+                    nc.scalar.activation(
+                        out=rows[:, h, :].rearrange("p (o c) -> p o c", o=2),
+                        in_=total[:, h],
+                        func=ACT.Copy,
+                        scale=factor[:, h : h + 1],
+                    )
                 return
             nc.gpsimd.tensor_tensor(
                 out=rows.rearrange("p h (o c) -> p h o c", o=2),
@@ -222,6 +206,30 @@ def tile_attention_pa_kernel(tc, x, freqs, Wq, Wk, Wv, mem_k, mem_v, out_q, out_
                 in1=by_half[:, :, :, 1, :],
                 op=ALU.add,
             )
+
+        def memory_rows():
+            mem_k_sq = keep.tile([HEADS, MEM_SLOTS, FEATURES], F32)
+            nc.scalar.activation(out=mem_k_sq[:], in_=mem_k_raw[:], func=ACT.Square)
+            mem_k_ss = keep.tile([HEADS, MEM_SLOTS], F32)
+            nc.vector.tensor_reduce(out=mem_k_ss[:], in_=mem_k_sq[:], axis=mybir.AxisListType.X, op=ALU.add)
+            mem_k_rsqrt = keep.tile([HEADS, MEM_SLOTS], F32)
+            nc.scalar.activation(out=mem_k_rsqrt[:], in_=mem_k_ss[:], func=ACT.Abs_reciprocal_sqrt)
+            mem_k_factor = keep.tile([HEADS, MEM_SLOTS], F32)
+            nc.vector.tensor_scalar_min(out=mem_k_factor[:], in0=mem_k_rsqrt[:], scalar1=1.0 / EPS)
+            mem_k_out = keep.tile([HEADS, MEM_SLOTS, FEATURES], F32)
+            nc.gpsimd.tensor_tensor(
+                out=mem_k_out[:],
+                in0=mem_k_raw[:],
+                in1=mem_k_factor[:].unsqueeze(2).to_broadcast([HEADS, MEM_SLOTS, FEATURES]),
+                op=ALU.mult,
+            )
+            mem_v_out = keep.tile([HEADS, MEM_SLOTS, FEATURES], F32)
+            nc.gpsimd.tensor_scalar(
+                out=mem_v_out[:], in0=mem_v_raw[:], scalar1=1.0, scalar2=0.0, op0=ALU.mult, op1=ALU.add
+            )
+            for b in range(BATCH):
+                nc.scalar.dma_start(out=out_k[b, :, 0:MEM_SLOTS, :], in_=mem_k_out[:])
+                nc.scalar.dma_start(out=out_v[b, :, 0:MEM_SLOTS, :], in_=mem_v_out[:])
 
         def store(w, part, b, first_tile, result):
             heads = slice(part * BANK_HEADS, (part + 1) * BANK_HEADS)
@@ -246,3 +254,5 @@ def tile_attention_pa_kernel(tc, x, freqs, Wq, Wk, Wv, mem_k, mem_v, out_q, out_
             project_and_rotate(w, part, token_tile, open_result[w][:, :, place, :])
             if place == TILES_PER_STORE - 1:
                 store(w, part, b, j - place, open_result[w])
+            if (w, unit) == (len(weights) - 1, TOKEN_TILES // 2):
+                memory_rows()

@@ -48,8 +48,8 @@ def tile_attention_pa_kernel(tc, x, freqs, Wq, Wk, Wv, mem_k, mem_v, out_q, out_
     with ExitStack() as ctx:
         keep = ctx.enter_context(tc.tile_pool(name="keep", bufs=1))
         stage = ctx.enter_context(tc.tile_pool(name="stage", bufs=2))
-        norms = ctx.enter_context(tc.tile_pool(name="norms", bufs=4))
-        rotated = ctx.enter_context(tc.tile_pool(name="rotated", bufs=4))
+        norms = ctx.enter_context(tc.tile_pool(name="norms", bufs=8))
+        rotated = ctx.enter_context(tc.tile_pool(name="rotated", bufs=8))
         results = ctx.enter_context(tc.tile_pool(name="results", bufs=3))
         psum_x = ctx.enter_context(tc.psum_pool(name="psum_x", bufs=2))
         psum_acc = ctx.enter_context(tc.psum_pool(name="psum_acc", bufs=6))
@@ -136,7 +136,7 @@ def tile_attention_pa_kernel(tc, x, freqs, Wq, Wk, Wv, mem_k, mem_v, out_q, out_
                 in_=w_grouped[:].rearrange("p g n t -> p (g n t)"),
             )
 
-        def project_and_rotate(w, part, token_tile, rows):
+        def project_and_rotate(w, part, token_tile, rows, added_by_tensor):
             r = w * PARTS + part
             acc = psum_acc.tile([P, BANK_COLUMNS], F32)
             for g in range(PASSES):
@@ -169,7 +169,6 @@ def tile_attention_pa_kernel(tc, x, freqs, Wq, Wk, Wv, mem_k, mem_v, out_q, out_
             products = rotated.tile(shape, F32)
             spread = acc[:].rearrange("p (h d) -> p h d", d=FEATURES).unsqueeze(2).to_broadcast(shape)
             factors_of_tile = table[:, token_tile % TILES_PER_BATCH].rearrange("p o a c -> p o (a c)")
-            added_by_tensor = w == 0 and token_tile % 2 == 0
             if normalised[w] and not added_by_tensor:
                 for h in range(BANK_HEADS):
                     nc.vector.scalar_tensor_tensor(
@@ -192,6 +191,9 @@ def tile_attention_pa_kernel(tc, x, freqs, Wq, Wk, Wv, mem_k, mem_v, out_q, out_
                 total = psum_x.tile([P, BANK_HEADS, 2, HALF], F32, name="aux")
                 for a in range(2):
                     nc.tensor.matmul(out=total[:], lhsT=identity[:], rhs=by_half[:, :, :, a, :], start=(a == 0), stop=(a == 1))
+                if not normalised[w]:
+                    nc.scalar.copy(out=rows.rearrange("p h (o c) -> p h o c", o=2), in_=total[:])
+                    return
                 for h in range(BANK_HEADS):
                     nc.scalar.activation(
                         out=rows[:, h, :].rearrange("p (o c) -> p o c", o=2),
@@ -245,13 +247,14 @@ def tile_attention_pa_kernel(tc, x, freqs, Wq, Wk, Wv, mem_k, mem_v, out_q, out_
                 quantise_w_range(w, part)
 
         open_result = [None] * len(weights)
-        for w, unit in banks:
+        for index, (w, unit) in enumerate(banks):
             part, token_tile = divmod(unit, TOKEN_TILES)
             b, j = divmod(token_tile, TILES_PER_BATCH)
             place = j % TILES_PER_STORE
             if place == 0:
                 open_result[w] = results.tile([P, BANK_HEADS, TILES_PER_STORE, FEATURES], F32, name="result%d" % w)
-            project_and_rotate(w, part, token_tile, open_result[w][:, :, place, :])
+            banks_behind = len(banks) - 1 - index
+            project_and_rotate(w, part, token_tile, open_result[w][:, :, place, :], banks_behind % 6 == 2)
             if place == TILES_PER_STORE - 1:
                 store(w, part, b, j - place, open_result[w])
             if (w, unit) == (len(weights) - 1, TOKEN_TILES // 2):

@@ -27,6 +27,9 @@ BANK_COLUMNS = 512
 BANK_HEADS = BANK_COLUMNS // FEATURES
 PARTS = HEADS // BANK_HEADS
 UNITS = PARTS * TOKEN_TILES
+PAIR = 2 * FEATURES
+PAIRS_PER_PART = BANK_COLUMNS // PAIR
+PAIRS_PER_STORE = 2
 WORDS_PER_PASS = K_PASS // 2
 
 FLOPS = 2 * BATCH * POSITIONS * DIM * 3 * HEADS * FEATURES
@@ -37,22 +40,26 @@ def tile_attention_pa_kernel(tc, x, freqs, Wq, Wk, Wv, mem_k, mem_v, out_q, out_
     weights = [Wq, Wk, Wv]
     outputs = [out_q, out_k, out_v]
     first_position = [0, MEM_SLOTS, MEM_SLOTS]
-    normalised = [True, True, False]
 
     banks = []
-    for step in range(UNITS + len(weights) - 1):
-        for w in range(len(weights)):
-            if 0 <= step - w < UNITS:
-                banks.append((w, step - w))
+    for step in range(UNITS + 3):
+        for w, behind in ((2, 0), (0, 2), (1, 3)):
+            if 0 <= step - behind < UNITS:
+                banks.append((w, step - behind))
+    arrivals = [("w", 2, 0)]
+    arrivals += [("x", t) for t in range(TILES_PER_BATCH)]
+    arrivals += [("w", 0, 0), ("x", 4), ("w", 1, 0), ("x", 5), ("x", 6), ("x", 7), ("w", 2, 1), ("w", 0, 1), ("w", 1, 1)]
 
     with ExitStack() as ctx:
         keep = ctx.enter_context(tc.tile_pool(name="keep", bufs=1))
         stage = ctx.enter_context(tc.tile_pool(name="stage", bufs=2))
         norms = ctx.enter_context(tc.tile_pool(name="norms", bufs=8))
-        rotated = ctx.enter_context(tc.tile_pool(name="rotated", bufs=8))
+        rotated = ctx.enter_context(tc.tile_pool(name="rotated", bufs=5))
+        rotated_v = ctx.enter_context(tc.tile_pool(name="rotated_v", bufs=3))
         results = ctx.enter_context(tc.tile_pool(name="results", bufs=3))
         psum_x = ctx.enter_context(tc.psum_pool(name="psum_x", bufs=2))
-        psum_acc = ctx.enter_context(tc.psum_pool(name="psum_acc", bufs=6))
+        psum_acc = ctx.enter_context(tc.psum_pool(name="psum_acc", bufs=4))
+        psum_acc_v = ctx.enter_context(tc.psum_pool(name="psum_acc_v", bufs=2))
 
         angles = keep.tile([P, TILES_PER_BATCH, 2, HALF], BF16)
         nc.scalar.dma_start(out=angles[:], in_=freqs.rearrange("(p j) (a c) -> p j a c", j=TILES_PER_BATCH, a=2))
@@ -66,14 +73,15 @@ def tile_attention_pa_kernel(tc, x, freqs, Wq, Wk, Wv, mem_k, mem_v, out_q, out_
             [keep.tile([P, PASSES, PACK, BANK_COLUMNS], BF16, name="w_raw%d_%d" % (w, part)) for part in range(PARTS)]
             for w in range(len(weights))
         ]
-        for w, unit in banks:
-            part, token_tile = divmod(unit, TOKEN_TILES)
-            if w == 0 and part == 0:
+        for arrival in arrivals:
+            if arrival[0] == "x":
+                token_tile = arrival[1]
                 b, j = divmod(token_tile, TILES_PER_BATCH)
                 nc.sync.dma_start(
                     out=x_raw[token_tile][:], in_=x[b].rearrange("(p j) k -> p j k", j=TILES_PER_BATCH)[:, j, :]
                 )
-            if token_tile == 0:
+            else:
+                w, part = arrival[1], arrival[2]
                 for g in (SCALAR_PASS, VECTOR_PASS):
                     nc.sync.dma_start(
                         out=w_raw[w][part][:, g],
@@ -84,6 +92,15 @@ def tile_attention_pa_kernel(tc, x, freqs, Wq, Wk, Wv, mem_k, mem_v, out_q, out_
 
         identity = keep.tile([P, P], F32)
         make_identity(nc, identity[:])
+        moves = keep.tile([P, 2, 2, FEATURES], F32)
+        for u in range(2):
+            straight = slice(u * FEATURES, (u + 1) * FEATURES)
+            nc.vector.tensor_copy(out=moves[:, u, u, :], in_=identity[:, straight])
+            for half in range(2):
+                source = (1 - u) * FEATURES + (1 - half) * HALF
+                nc.vector.tensor_copy(
+                    out=moves[:, u, 1 - u, half * HALF : (half + 1) * HALF], in_=identity[:, source : source + HALF]
+                )
 
         table = keep.tile([P, TILES_PER_BATCH, 2, 2, HALF], F32)
         nc.scalar.activation(out=table[:, :, 1, 0, :], in_=angles[:, :, 1, :], func=ACT.Sin)
@@ -96,9 +113,17 @@ def tile_attention_pa_kernel(tc, x, freqs, Wq, Wk, Wv, mem_k, mem_v, out_q, out_
             nc.vector.tensor_scalar(
                 out=table[:, :, a, a, :], in0=half_sin_sq[:, :, a, :], scalar1=-2.0, scalar2=1.0, op0=ALU.mult, op1=ALU.add
             )
+        blocks = keep.tile([P, TILES_PER_BATCH, 6, HALF], F32)
+        nc.scalar.activation(out=blocks[:, :, 2, :], in_=angles[:, :, 1, :], func=ACT.Sin)
+        nc.scalar.activation(out=blocks[:, :, 3, :], in_=angles[:, :, 0, :], func=ACT.Sin, scale=-1.0)
+        for first in (0, 4):
+            nc.vector.tensor_scalar(
+                out=blocks[:, :, first : first + 2, :], in0=half_sin_sq[:], scalar1=-2.0, scalar2=1.0, op0=ALU.mult, op1=ALU.add
+            )
+        turned_table = keep.tile([P, 2, POSITIONS], F32)
 
-        x_codes = keep.tile([P, TOKEN_TILES, PASSES * P], U32, align_bytes=64)
-        x_scales = keep.tile([P, TOKEN_TILES, PASSES * P], U8, align_bytes=64)
+        x_codes = keep.tile([P, BATCH, PASSES, POSITIONS], U32, align_bytes=64)
+        x_scales = keep.tile([P, BATCH, PASSES, POSITIONS], U8, align_bytes=64)
         w_codes = keep.tile([P, len(weights) * PARTS, PASSES * BANK_COLUMNS], U32, align_bytes=64)
         w_scales = keep.tile([P, len(weights) * PARTS, PASSES * BANK_COLUMNS], U8, align_bytes=64)
 
@@ -116,8 +141,61 @@ def tile_attention_pa_kernel(tc, x, freqs, Wq, Wk, Wv, mem_k, mem_v, out_q, out_
                 out=x_grouped[:].bitcast(F32).rearrange("p (g r u) -> p g r u", g=PASSES, u=2),
                 in_=transposed[:].rearrange("p (g u) r -> p g r u", g=PASSES),
             )
-            nc.vector.quantize_mx(
-                out=x_codes[:, token_tile, :].bitcast(FP8X4), scales=x_scales[:, token_tile, :], in_=x_grouped[:]
+            b, j = divmod(token_tile, TILES_PER_BATCH)
+            tokens = slice(j * P, (j + 1) * P)
+            for g in range(PASSES):
+                nc.vector.quantize_mx(
+                    out=x_codes[:, b, g, tokens].bitcast(FP8X4),
+                    scales=x_scales[:, b, g, tokens],
+                    in_=x_grouped[:, g * P * PACK : (g + 1) * P * PACK],
+                )
+
+        def turn_table():
+            for u in range(2):
+                turned = psum_x.tile([P, POSITIONS], F32, name="aux")
+                for j in range(TILES_PER_BATCH):
+                    nc.tensor.transpose(
+                        turned[:, j * P : (j + 1) * P],
+                        blocks[:, j, 2 * u : 2 * u + 4, :].rearrange("p b c -> p (b c)"),
+                        identity[:],
+                    )
+                if u == 0:
+                    nc.scalar.copy(out=turned_table[:, u, :], in_=turned[:])
+                else:
+                    nc.vector.tensor_copy(out=turned_table[:, u, :], in_=turned[:])
+
+        def project_and_rotate_v(part, b, pair, rows):
+            r = 2 * PARTS + part
+            acc = psum_acc_v.tile([P, BANK_COLUMNS], F32, name="acc")
+            for g in range(PASSES):
+                columns = slice(g * BANK_COLUMNS + pair * PAIR, g * BANK_COLUMNS + (pair + 1) * PAIR)
+                nc.tensor.matmul_mx(
+                    out=acc[:],
+                    lhsT=w_codes[:, r, columns].bitcast(FP8X4),
+                    lhsT_scale=w_scales[:, r, columns],
+                    rhs=x_codes[:, b, g, :].bitcast(FP8X4),
+                    rhs_scale=x_scales[:, b, g, :],
+                    start=(g == 0),
+                    stop=(g == PASSES - 1),
+                )
+            shape = [P, 2, POSITIONS]
+            products = rotated_v.tile(shape, F32, name="products")
+            nc.vector.tensor_tensor(
+                out=products[:], in0=acc[:].unsqueeze(1).to_broadcast(shape), in1=turned_table[:], op=ALU.mult
+            )
+            total = psum_x.tile([P, TILES_PER_BATCH, PAIR], F32, name="aux")
+            for j in range(TILES_PER_BATCH):
+                for u in range(2):
+                    nc.tensor.matmul(
+                        out=total[:, j, :],
+                        lhsT=products[:, u, j * P : (j + 1) * P],
+                        rhs=moves[:, u].rearrange("p h d -> p (h d)"),
+                        is_transpose=True,
+                        start=(u == 0),
+                        stop=(u == 1),
+                    )
+            nc.scalar.copy(
+                out=rows.rearrange("p h j d -> p j h d"), in_=total[:].rearrange("p j (h d) -> p j h d", h=2)
             )
 
         def quantise_w_range(w, part):
@@ -136,72 +214,49 @@ def tile_attention_pa_kernel(tc, x, freqs, Wq, Wk, Wv, mem_k, mem_v, out_q, out_
                 in_=w_grouped[:].rearrange("p g n t -> p (g n t)"),
             )
 
-        def project_and_rotate(w, part, token_tile, rows, added_by_tensor):
+        def project_and_rotate(w, part, token_tile, rows):
             r = w * PARTS + part
-            acc = psum_acc.tile([P, BANK_COLUMNS], F32)
+            b, j = divmod(token_tile, TILES_PER_BATCH)
+            acc = psum_acc.tile([P, BANK_COLUMNS], F32, name="acc")
             for g in range(PASSES):
-                tokens = slice(g * P, (g + 1) * P)
+                tokens = slice(j * P, (j + 1) * P)
                 columns = slice(g * BANK_COLUMNS, (g + 1) * BANK_COLUMNS)
                 nc.tensor.matmul_mx(
                     out=acc[:],
-                    lhsT=x_codes[:, token_tile, tokens].bitcast(FP8X4),
-                    lhsT_scale=x_scales[:, token_tile, tokens],
+                    lhsT=x_codes[:, b, g, tokens].bitcast(FP8X4),
+                    lhsT_scale=x_scales[:, b, g, tokens],
                     rhs=w_codes[:, r, columns].bitcast(FP8X4),
                     rhs_scale=w_scales[:, r, columns],
                     start=(g == 0),
                     stop=(g == PASSES - 1),
                 )
-            if normalised[w]:
-                squares = stage.tile([P, BANK_HEADS, FEATURES], F32)
-                sum_sq = norms.tile([P, BANK_HEADS], F32)
-                for h in range(BANK_HEADS):
-                    nc.scalar.activation(
-                        out=squares[:, h, :],
-                        in_=acc[:, h * FEATURES : (h + 1) * FEATURES],
-                        func=ACT.Square,
-                        accum_out=sum_sq[:, h : h + 1],
-                    )
-                above = norms.tile([P, BANK_HEADS], F32)
-                nc.scalar.activation(out=above[:], in_=sum_sq[:], func=ACT.Relu, bias=-EPS * EPS)
-                factor = norms.tile([P, BANK_HEADS], F32)
-                nc.scalar.activation(out=factor[:], in_=above[:], func=ACT.Abs_reciprocal_sqrt, bias=EPS * EPS)
+            squares = stage.tile([P, BANK_HEADS, FEATURES], F32)
+            sum_sq = norms.tile([P, BANK_HEADS], F32)
+            for h in range(BANK_HEADS):
+                nc.scalar.activation(
+                    out=squares[:, h, :],
+                    in_=acc[:, h * FEATURES : (h + 1) * FEATURES],
+                    func=ACT.Square,
+                    accum_out=sum_sq[:, h : h + 1],
+                )
+            above = norms.tile([P, BANK_HEADS], F32)
+            nc.scalar.activation(out=above[:], in_=sum_sq[:], func=ACT.Relu, bias=-EPS * EPS)
+            factor = norms.tile([P, BANK_HEADS], F32)
+            nc.scalar.activation(out=factor[:], in_=above[:], func=ACT.Abs_reciprocal_sqrt, bias=EPS * EPS)
             shape = [P, BANK_HEADS, 2, FEATURES]
-            products = rotated.tile(shape, F32)
+            products = rotated.tile(shape, F32, name="products")
             spread = acc[:].rearrange("p (h d) -> p h d", d=FEATURES).unsqueeze(2).to_broadcast(shape)
-            factors_of_tile = table[:, token_tile % TILES_PER_BATCH].rearrange("p o a c -> p o (a c)")
-            if normalised[w] and not added_by_tensor:
-                for h in range(BANK_HEADS):
-                    nc.vector.scalar_tensor_tensor(
-                        out=products[:, h],
-                        in0=spread[:, h],
-                        scalar=factor[:, h : h + 1],
-                        in1=factors_of_tile,
-                        op0=ALU.mult,
-                        op1=ALU.mult,
-                    )
-            else:
-                nc.vector.tensor_tensor(
-                    out=products[:],
-                    in0=spread,
-                    in1=factors_of_tile.unsqueeze(1).to_broadcast(shape),
-                    op=ALU.mult,
+            factors_of_tile = table[:, j].rearrange("p o a c -> p o (a c)")
+            for h in range(BANK_HEADS):
+                nc.vector.scalar_tensor_tensor(
+                    out=products[:, h],
+                    in0=spread[:, h],
+                    scalar=factor[:, h : h + 1],
+                    in1=factors_of_tile,
+                    op0=ALU.mult,
+                    op1=ALU.mult,
                 )
             by_half = products[:].rearrange("p h o (a c) -> p h o a c", a=2)
-            if added_by_tensor:
-                total = psum_x.tile([P, BANK_HEADS, 2, HALF], F32, name="aux")
-                for a in range(2):
-                    nc.tensor.matmul(out=total[:], lhsT=identity[:], rhs=by_half[:, :, :, a, :], start=(a == 0), stop=(a == 1))
-                if not normalised[w]:
-                    nc.scalar.copy(out=rows.rearrange("p h (o c) -> p h o c", o=2), in_=total[:])
-                    return
-                for h in range(BANK_HEADS):
-                    nc.scalar.activation(
-                        out=rows[:, h, :].rearrange("p (o c) -> p o c", o=2),
-                        in_=total[:, h],
-                        func=ACT.Copy,
-                        scale=factor[:, h : h + 1],
-                    )
-                return
             nc.gpsimd.tensor_tensor(
                 out=rows.rearrange("p h (o c) -> p h o c", o=2),
                 in0=by_half[:, :, :, 0, :],
@@ -239,23 +294,37 @@ def tile_attention_pa_kernel(tc, x, freqs, Wq, Wk, Wv, mem_k, mem_v, out_q, out_
             by_tile = outputs[w][b, heads, positions, :].rearrange("h (p j) d -> p h j d", j=TILES_PER_BATCH)
             nc.sync.dma_start(out=by_tile[:, :, first_tile : first_tile + TILES_PER_STORE, :], in_=result[:])
 
-        for w, unit in banks:
-            part, token_tile = divmod(unit, TOKEN_TILES)
-            if w == 0 and part == 0:
-                quantise_x_tile(token_tile)
-            if token_tile == 0:
-                quantise_w_range(w, part)
+        for arrival in arrivals:
+            if arrival[0] == "x":
+                quantise_x_tile(arrival[1])
+            else:
+                quantise_w_range(arrival[1], arrival[2])
+            if arrival == ("w", 2, 0):
+                turn_table()
 
         open_result = [None] * len(weights)
-        for index, (w, unit) in enumerate(banks):
-            part, token_tile = divmod(unit, TOKEN_TILES)
-            b, j = divmod(token_tile, TILES_PER_BATCH)
-            place = j % TILES_PER_STORE
-            if place == 0:
-                open_result[w] = results.tile([P, BANK_HEADS, TILES_PER_STORE, FEATURES], F32, name="result%d" % w)
-            banks_behind = len(banks) - 1 - index
-            project_and_rotate(w, part, token_tile, open_result[w][:, :, place, :], banks_behind % 6 == 2)
-            if place == TILES_PER_STORE - 1:
-                store(w, part, b, j - place, open_result[w])
+        for w, unit in banks:
+            part, place_in_part = divmod(unit, TOKEN_TILES)
+            if w < 2:
+                b, j = divmod(place_in_part, TILES_PER_BATCH)
+                place = j % TILES_PER_STORE
+                if place == 0:
+                    open_result[w] = results.tile([P, BANK_HEADS, TILES_PER_STORE, FEATURES], F32, name="result%d" % w)
+                project_and_rotate(w, part, place_in_part, open_result[w][:, :, place, :])
+                if place == TILES_PER_STORE - 1:
+                    store(w, part, b, j - place, open_result[w])
+            else:
+                b, pair = divmod(place_in_part, PAIRS_PER_PART)
+                place = pair % PAIRS_PER_STORE
+                if place == 0:
+                    open_result[w] = results.tile([P, 2 * PAIRS_PER_STORE, TILES_PER_BATCH, FEATURES], F32, name="result2")
+                project_and_rotate_v(part, b, pair, open_result[w][:, 2 * place : 2 * place + 2])
+                if place == PAIRS_PER_STORE - 1:
+                    first_head = part * BANK_HEADS + 2 * (pair - place)
+                    rows_of_heads = out_v[b, first_head : first_head + 2 * PAIRS_PER_STORE, MEM_SLOTS : MEM_SLOTS + POSITIONS, :]
+                    nc.sync.dma_start(
+                        out=rows_of_heads.rearrange("h (p j) d -> p h (j d)", j=TILES_PER_BATCH),
+                        in_=open_result[w][:].rearrange("p h j d -> p h (j d)"),
+                    )
             if (w, unit) == (len(weights) - 1, TOKEN_TILES // 2):
                 memory_rows()

@@ -19,7 +19,8 @@ P = 128
 PACK = 4
 K_PASS = P * PACK
 PASSES = DIM // K_PASS
-VECTOR_PASS, SCALAR_PASS = 0, 1
+Q, K, V = 0, 1, 2
+EARLY_V = 4
 TILES_PER_BATCH = POSITIONS // P
 TOKEN_TILES = BATCH * TILES_PER_BATCH
 TILES_PER_STORE = 2
@@ -41,25 +42,14 @@ def tile_attention_pa_kernel(tc, x, freqs, Wq, Wk, Wv, mem_k, mem_v, out_q, out_
     outputs = [out_q, out_k, out_v]
     first_position = [0, MEM_SLOTS, MEM_SLOTS]
 
-    banks = []
-    for step in range(UNITS + 3):
-        for w, behind in ((2, 0), (0, 2), (1, 3)):
-            if 0 <= step - behind < UNITS:
-                banks.append((w, step - behind))
-    arrivals = [("w", 2, 0)]
-    arrivals += [("x", t) for t in range(TILES_PER_BATCH)]
-    arrivals += [("w", 0, 0), ("x", 4), ("w", 1, 0), ("x", 5), ("x", 6), ("x", 7), ("w", 2, 1), ("w", 0, 1), ("w", 1, 1)]
-
     with ExitStack() as ctx:
         keep = ctx.enter_context(tc.tile_pool(name="keep", bufs=1))
         stage = ctx.enter_context(tc.tile_pool(name="stage", bufs=2))
         norms = ctx.enter_context(tc.tile_pool(name="norms", bufs=8))
-        rotated = ctx.enter_context(tc.tile_pool(name="rotated", bufs=5))
-        rotated_v = ctx.enter_context(tc.tile_pool(name="rotated_v", bufs=3))
+        rotated = ctx.enter_context(tc.tile_pool(name="rotated", bufs=8))
         results = ctx.enter_context(tc.tile_pool(name="results", bufs=3))
-        psum_x = ctx.enter_context(tc.psum_pool(name="psum_x", bufs=2))
-        psum_acc = ctx.enter_context(tc.psum_pool(name="psum_acc", bufs=4))
-        psum_acc_v = ctx.enter_context(tc.psum_pool(name="psum_acc_v", bufs=2))
+        psum_aux = ctx.enter_context(tc.psum_pool(name="psum_aux", bufs=2))
+        psum_acc = ctx.enter_context(tc.psum_pool(name="psum_acc", bufs=6))
 
         angles = keep.tile([P, TILES_PER_BATCH, 2, HALF], BF16)
         nc.scalar.dma_start(out=angles[:], in_=freqs.rearrange("(p j) (a c) -> p j a c", j=TILES_PER_BATCH, a=2))
@@ -73,22 +63,30 @@ def tile_attention_pa_kernel(tc, x, freqs, Wq, Wk, Wv, mem_k, mem_v, out_q, out_
             [keep.tile([P, PASSES, PACK, BANK_COLUMNS], BF16, name="w_raw%d_%d" % (w, part)) for part in range(PARTS)]
             for w in range(len(weights))
         ]
-        for arrival in arrivals:
-            if arrival[0] == "x":
-                token_tile = arrival[1]
-                b, j = divmod(token_tile, TILES_PER_BATCH)
+
+        def load_x(token_tile):
+            b, j = divmod(token_tile, TILES_PER_BATCH)
+            nc.sync.dma_start(
+                out=x_raw[token_tile][:], in_=x[b].rearrange("(p j) k -> p j k", j=TILES_PER_BATCH)[:, j, :]
+            )
+
+        def load_w(w, part):
+            for g in range(PASSES):
                 nc.sync.dma_start(
-                    out=x_raw[token_tile][:], in_=x[b].rearrange("(p j) k -> p j k", j=TILES_PER_BATCH)[:, j, :]
+                    out=w_raw[w][part][:, g],
+                    in_=weights[w][
+                        g * K_PASS : (g + 1) * K_PASS, part * BANK_COLUMNS : (part + 1) * BANK_COLUMNS
+                    ].rearrange("(p t) n -> p t n", t=PACK),
                 )
-            else:
-                w, part = arrival[1], arrival[2]
-                for g in (SCALAR_PASS, VECTOR_PASS):
-                    nc.sync.dma_start(
-                        out=w_raw[w][part][:, g],
-                        in_=weights[w][
-                            g * K_PASS : (g + 1) * K_PASS, part * BANK_COLUMNS : (part + 1) * BANK_COLUMNS
-                        ].rearrange("(p t) n -> p t n", t=PACK),
-                    )
+
+        for token_tile in range(TILES_PER_BATCH):
+            load_x(token_tile)
+        for w in (V, Q, K):
+            load_w(w, 0)
+        for token_tile in range(TILES_PER_BATCH, TOKEN_TILES):
+            load_x(token_tile)
+        for w in (V, Q, K):
+            load_w(w, 1)
 
         identity = keep.tile([P, P], F32)
         make_identity(nc, identity[:])
@@ -102,88 +100,212 @@ def tile_attention_pa_kernel(tc, x, freqs, Wq, Wk, Wv, mem_k, mem_v, out_q, out_
                     out=moves[:, u, 1 - u, half * HALF : (half + 1) * HALF], in_=identity[:, source : source + HALF]
                 )
 
-        table = keep.tile([P, TILES_PER_BATCH, 2, 2, HALF], F32)
-        nc.scalar.activation(out=table[:, :, 1, 0, :], in_=angles[:, :, 1, :], func=ACT.Sin)
-        nc.scalar.activation(out=table[:, :, 0, 1, :], in_=angles[:, :, 0, :], func=ACT.Sin, scale=-1.0)
         half_sin = keep.tile([P, TILES_PER_BATCH, 2, HALF], F32)
         nc.scalar.activation(out=half_sin[:], in_=angles[:], func=ACT.Sin, scale=0.5)
+        table = keep.tile([P, TILES_PER_BATCH, 2, 2, HALF], F32)
+        blocks = keep.tile([P, TILES_PER_BATCH, 6, HALF], F32)
+        for target in (blocks[:, :, 2, :], table[:, :, 1, 0, :]):
+            nc.scalar.activation(out=target, in_=angles[:, :, 1, :], func=ACT.Sin)
+        for target in (blocks[:, :, 3, :], table[:, :, 0, 1, :]):
+            nc.scalar.activation(out=target, in_=angles[:, :, 0, :], func=ACT.Sin, scale=-1.0)
+        ones = keep.tile([P, 1], F32)
+        nc.vector.memset(ones[:], 1.0)
+        inverse_of_one = keep.tile([P, 1], F32)
+        nc.scalar.activation(out=inverse_of_one[:], in_=ones[:], func=ACT.Abs_reciprocal_sqrt)
         half_sin_sq = keep.tile([P, TILES_PER_BATCH, 2, HALF], F32)
         nc.vector.tensor_tensor(out=half_sin_sq[:], in0=half_sin[:], in1=half_sin[:], op=ALU.mult)
-        for a in range(2):
-            nc.vector.tensor_scalar(
-                out=table[:, :, a, a, :], in0=half_sin_sq[:, :, a, :], scalar1=-2.0, scalar2=1.0, op0=ALU.mult, op1=ALU.add
-            )
-        blocks = keep.tile([P, TILES_PER_BATCH, 6, HALF], F32)
-        nc.scalar.activation(out=blocks[:, :, 2, :], in_=angles[:, :, 1, :], func=ACT.Sin)
-        nc.scalar.activation(out=blocks[:, :, 3, :], in_=angles[:, :, 0, :], func=ACT.Sin, scale=-1.0)
         for first in (0, 4):
             nc.vector.tensor_scalar(
                 out=blocks[:, :, first : first + 2, :], in0=half_sin_sq[:], scalar1=-2.0, scalar2=1.0, op0=ALU.mult, op1=ALU.add
             )
+        for a in range(2):
+            nc.vector.tensor_scalar(
+                out=table[:, :, a, a, :], in0=half_sin_sq[:, :, a, :], scalar1=-2.0, scalar2=1.0, op0=ALU.mult, op1=ALU.add
+            )
         turned_table = keep.tile([P, 2, POSITIONS], F32)
 
-        x_codes = keep.tile([P, BATCH, PASSES, POSITIONS], U32, align_bytes=64)
-        x_scales = keep.tile([P, BATCH, PASSES, POSITIONS], U8, align_bytes=64)
+        x_codes = keep.tile([P, BATCH, PASSES * POSITIONS], U32, align_bytes=64)
+        x_scales = keep.tile([P, BATCH, PASSES * POSITIONS], U8, align_bytes=64)
         w_codes = keep.tile([P, len(weights) * PARTS, PASSES * BANK_COLUMNS], U32, align_bytes=64)
         w_scales = keep.tile([P, len(weights) * PARTS, PASSES * BANK_COLUMNS], U8, align_bytes=64)
+        x_grouped = [None] * BATCH
+        w_grouped = [None] * (len(weights) * PARTS)
 
-        def quantise_x_tile(token_tile):
+        def transpose_x_tile(token_tile):
+            b, j = divmod(token_tile, TILES_PER_BATCH)
+            if j == 0:
+                x_grouped[b] = keep.tile([P, PASSES, POSITIONS * PACK], BF16, name="x_grouped%d" % b, align_bytes=64)
             words = x_raw[token_tile][:].bitcast(F32)
-            transposed = psum_x.tile([P, PASSES * 2, P], F32, name="aux")
+            transposed = psum_aux.tile([P, PASSES * 2, P], F32, name="aux")
             for g in range(PASSES):
                 for u in range(2):
                     first_word = g * WORDS_PER_PASS + u
                     nc.tensor.transpose(
                         transposed[:, 2 * g + u, :], words[:, first_word : first_word + WORDS_PER_PASS - 1 : 2], identity[:]
                     )
-            x_grouped = stage.tile([P, PASSES * P * PACK], BF16, align_bytes=64)
+            rows = x_grouped[b][:, :, j * P * PACK : (j + 1) * P * PACK]
             nc.scalar.copy(
-                out=x_grouped[:].bitcast(F32).rearrange("p (g r u) -> p g r u", g=PASSES, u=2),
+                out=rows.bitcast(F32).rearrange("p g (r u) -> p g r u", u=2),
                 in_=transposed[:].rearrange("p (g u) r -> p g r u", g=PASSES),
             )
-            b, j = divmod(token_tile, TILES_PER_BATCH)
-            tokens = slice(j * P, (j + 1) * P)
-            for g in range(PASSES):
-                nc.vector.quantize_mx(
-                    out=x_codes[:, b, g, tokens].bitcast(FP8X4),
-                    scales=x_scales[:, b, g, tokens],
-                    in_=x_grouped[:, g * P * PACK : (g + 1) * P * PACK],
+
+        def quantise_x(b):
+            nc.vector.quantize_mx(
+                out=x_codes[:, b, :].bitcast(FP8X4),
+                scales=x_scales[:, b, :],
+                in_=x_grouped[b][:].rearrange("p g n -> p (g n)"),
+            )
+
+        turned = [None, None]
+
+        def turn_table(u):
+            turned[u] = psum_aux.tile([P, POSITIONS], F32, name="aux")
+            for j in range(TILES_PER_BATCH):
+                nc.tensor.transpose(
+                    turned[u][:, j * P : (j + 1) * P],
+                    blocks[:, j, 2 * u : 2 * u + 4, :].rearrange("p b c -> p (b c)"),
+                    identity[:],
                 )
 
-        def turn_table():
-            for u in range(2):
-                turned = psum_x.tile([P, POSITIONS], F32, name="aux")
-                for j in range(TILES_PER_BATCH):
-                    nc.tensor.transpose(
-                        turned[:, j * P : (j + 1) * P],
-                        blocks[:, j, 2 * u : 2 * u + 4, :].rearrange("p b c -> p (b c)"),
-                        identity[:],
-                    )
-                if u == 0:
-                    nc.scalar.copy(out=turned_table[:, u, :], in_=turned[:])
-                else:
-                    nc.vector.tensor_copy(out=turned_table[:, u, :], in_=turned[:])
+        def open_grouped(w, part):
+            by_scalar = stage.tile([P, BANK_COLUMNS, PACK], BF16, name="by_scalar", align_bytes=64)
+            by_other = keep.tile([P, BANK_COLUMNS, PACK], BF16, name="by_other", align_bytes=64)
+            w_grouped[w * PARTS + part] = [by_scalar, by_other]
 
-        def project_and_rotate_v(part, b, pair, rows):
-            r = 2 * PARTS + part
-            acc = psum_acc_v.tile([P, BANK_COLUMNS], F32, name="acc")
+        def lay_by_scalar(w, part, columns):
+            nc.scalar.copy(
+                out=w_grouped[w * PARTS + part][0][:, columns].rearrange("p (c i) t -> p c t i", i=4),
+                in_=w_raw[w][part][:, 0, :, columns].rearrange("p t (c i) -> p c t i", i=4),
+            )
+
+        def lay_by_vector(w, part, columns):
+            nc.vector.tensor_copy(
+                out=w_grouped[w * PARTS + part][1][:, columns].rearrange("p (c i) t -> p c t i", i=4),
+                in_=w_raw[w][part][:, 1, :, columns].rearrange("p t (c i) -> p c t i", i=4),
+            )
+
+        def lay_by_gpsimd(w, part, columns):
+            nc.gpsimd.tensor_scalar(
+                out=w_grouped[w * PARTS + part][1][:, columns],
+                in0=w_raw[w][part][:, 1, :, columns].rearrange("p t n -> p n t"),
+                scalar1=1.0,
+                scalar2=0.0,
+                op0=ALU.mult,
+                op1=ALU.add,
+            )
+
+        def quantise_w(w, part):
+            r = w * PARTS + part
             for g in range(PASSES):
-                columns = slice(g * BANK_COLUMNS + pair * PAIR, g * BANK_COLUMNS + (pair + 1) * PAIR)
+                columns = slice(g * BANK_COLUMNS, (g + 1) * BANK_COLUMNS)
+                nc.vector.quantize_mx(
+                    out=w_codes[:, r, columns].bitcast(FP8X4),
+                    scales=w_scales[:, r, columns],
+                    in_=w_grouped[r][g][:].rearrange("p n t -> p (n t)"),
+                )
+
+        state = {}
+        open_result = [None] * len(weights)
+
+        def matmuls(item):
+            w, unit = item
+            part, place_in_part = divmod(unit, TOKEN_TILES)
+            b, place = divmod(place_in_part, TILES_PER_BATCH)
+            r = w * PARTS + part
+            acc = psum_acc.tile([P, BANK_COLUMNS], F32, name="acc")
+            state[item] = {"acc": acc}
+            for g in range(PASSES):
+                if w == V:
+                    tokens = slice(g * POSITIONS, (g + 1) * POSITIONS)
+                    columns = slice(g * BANK_COLUMNS + place * PAIR, g * BANK_COLUMNS + (place + 1) * PAIR)
+                    still, moving = (w_codes[:, r, columns], w_scales[:, r, columns]), (x_codes[:, b, tokens], x_scales[:, b, tokens])
+                else:
+                    tokens = slice(g * POSITIONS + place * P, g * POSITIONS + (place + 1) * P)
+                    columns = slice(g * BANK_COLUMNS, (g + 1) * BANK_COLUMNS)
+                    still, moving = (x_codes[:, b, tokens], x_scales[:, b, tokens]), (w_codes[:, r, columns], w_scales[:, r, columns])
                 nc.tensor.matmul_mx(
                     out=acc[:],
-                    lhsT=w_codes[:, r, columns].bitcast(FP8X4),
-                    lhsT_scale=w_scales[:, r, columns],
-                    rhs=x_codes[:, b, g, :].bitcast(FP8X4),
-                    rhs_scale=x_scales[:, b, g, :],
+                    lhsT=still[0].bitcast(FP8X4),
+                    lhsT_scale=still[1],
+                    rhs=moving[0].bitcast(FP8X4),
+                    rhs_scale=moving[1],
                     start=(g == 0),
                     stop=(g == PASSES - 1),
                 )
-            shape = [P, 2, POSITIONS]
-            products = rotated_v.tile(shape, F32, name="products")
-            nc.vector.tensor_tensor(
-                out=products[:], in0=acc[:].unsqueeze(1).to_broadcast(shape), in1=turned_table[:], op=ALU.mult
+
+        def sum_squares(item, heads):
+            acc = state[item]["acc"]
+            if heads[0] == 0:
+                state[item]["sum_sq"] = norms.tile([P, BANK_HEADS], F32, name="sum_sq")
+                state[item]["squares"] = stage.tile([P, BANK_HEADS, FEATURES], F32, name="squares")
+            for h in heads:
+                nc.scalar.activation(
+                    out=state[item]["squares"][:, h, :],
+                    in_=acc[:, h * FEATURES : (h + 1) * FEATURES],
+                    func=ACT.Square,
+                    accum_out=state[item]["sum_sq"][:, h : h + 1],
+                )
+
+        def clip(item):
+            above = norms.tile([P, BANK_HEADS], F32, name="above")
+            state[item]["above"] = above
+            nc.scalar.activation(out=above[:], in_=state[item]["sum_sq"][:], func=ACT.Relu, bias=-EPS * EPS)
+
+        def invert(item):
+            factor = norms.tile([P, BANK_HEADS], F32, name="factor")
+            state[item]["factor"] = factor
+            nc.scalar.activation(out=factor[:], in_=state[item]["above"][:], func=ACT.Abs_reciprocal_sqrt, bias=EPS * EPS)
+
+        def multiply(item):
+            w, unit = item
+            acc = state[item]["acc"]
+            products = rotated.tile([P, 2 * BANK_COLUMNS], F32, name="products")
+            state[item]["products"] = products
+            if w == V:
+                shape = [P, 2, POSITIONS]
+                nc.vector.tensor_tensor(
+                    out=products[:].rearrange("p (u n) -> p u n", u=2),
+                    in0=acc[:].unsqueeze(1).to_broadcast(shape),
+                    in1=turned_table[:],
+                    op=ALU.mult,
+                )
+                return
+            by_head = products[:].rearrange("p (h o d) -> p h o d", h=BANK_HEADS, o=2)
+            spread = acc[:].rearrange("p (h d) -> p h d", d=FEATURES).unsqueeze(2).to_broadcast([P, BANK_HEADS, 2, FEATURES])
+            for h in range(BANK_HEADS):
+                nc.vector.scalar_tensor_tensor(
+                    out=by_head[:, h],
+                    in0=spread[:, h],
+                    scalar=state[item]["factor"][:, h : h + 1],
+                    in1=table[:, unit % TILES_PER_BATCH].rearrange("p o a c -> p o (a c)"),
+                    op0=ALU.mult,
+                    op1=ALU.mult,
+                )
+
+        def add(item):
+            w, unit = item
+            place = unit % TILES_PER_STORE
+            if place == 0:
+                open_result[w] = results.tile([P, BANK_HEADS, TILES_PER_STORE, FEATURES], F32, name="result%d" % w)
+            by_half = state[item]["products"][:].rearrange("p (h o a c) -> p h o a c", h=BANK_HEADS, o=2, a=2)
+            nc.gpsimd.tensor_tensor(
+                out=open_result[w][:, :, place, :].rearrange("p h (o c) -> p h o c", o=2),
+                in0=by_half[:, :, :, 0, :],
+                in1=by_half[:, :, :, 1, :],
+                op=ALU.add,
             )
-            total = psum_x.tile([P, TILES_PER_BATCH, PAIR], F32, name="aux")
+            if place == TILES_PER_STORE - 1:
+                part, place_in_part = divmod(unit, TOKEN_TILES)
+                b, j = divmod(place_in_part, TILES_PER_BATCH)
+                heads = slice(part * BANK_HEADS, (part + 1) * BANK_HEADS)
+                positions = slice(first_position[w], first_position[w] + POSITIONS)
+                by_tile = outputs[w][b, heads, positions, :].rearrange("h (p j) d -> p h j d", j=TILES_PER_BATCH)
+                nc.sync.dma_start(out=by_tile[:, :, j - place : j + 1, :], in_=open_result[w][:])
+
+        def turn_back(item):
+            products = state[item]["products"][:].rearrange("p (u n) -> p u n", u=2)
+            total = psum_aux.tile([P, TILES_PER_BATCH, PAIR], F32, name="aux")
+            state[item]["total"] = total
             for j in range(TILES_PER_BATCH):
                 for u in range(2):
                     nc.tensor.matmul(
@@ -194,137 +316,140 @@ def tile_attention_pa_kernel(tc, x, freqs, Wq, Wk, Wv, mem_k, mem_v, out_q, out_
                         start=(u == 0),
                         stop=(u == 1),
                     )
+
+        def copy_back(item):
+            w, unit = item
+            part, place_in_part = divmod(unit, TOKEN_TILES)
+            b, pair = divmod(place_in_part, PAIRS_PER_PART)
+            place = pair % PAIRS_PER_STORE
+            if place == 0:
+                open_result[w] = results.tile([P, 2 * PAIRS_PER_STORE, TILES_PER_BATCH, FEATURES], F32, name="result2")
             nc.scalar.copy(
-                out=rows.rearrange("p h j d -> p j h d"), in_=total[:].rearrange("p j (h d) -> p j h d", h=2)
+                out=open_result[w][:, 2 * place : 2 * place + 2].rearrange("p h j d -> p j h d"),
+                in_=state[item]["total"][:].rearrange("p j (h d) -> p j h d", h=2),
             )
+            if place == PAIRS_PER_STORE - 1:
+                first_head = part * BANK_HEADS + 2 * (pair - place)
+                rows_of_heads = out_v[b, first_head : first_head + 2 * PAIRS_PER_STORE, MEM_SLOTS : MEM_SLOTS + POSITIONS, :]
+                nc.sync.dma_start(
+                    out=rows_of_heads.rearrange("h (p j) d -> p h (j d)", j=TILES_PER_BATCH),
+                    in_=open_result[w][:].rearrange("p h j d -> p h (j d)"),
+                )
 
-        def quantise_w_range(w, part):
-            r = w * PARTS + part
-            w_grouped = stage.tile([P, PASSES, BANK_COLUMNS, PACK], BF16, align_bytes=64)
-            for g in (SCALAR_PASS, VECTOR_PASS):
-                source = w_raw[w][part][:, g].rearrange("p t (c i) -> p c t i", i=4)
-                target = w_grouped[:, g].rearrange("p (c i) t -> p c t i", i=4)
-                if g == VECTOR_PASS:
-                    nc.vector.tensor_copy(out=target, in_=source)
-                else:
-                    nc.scalar.copy(out=target, in_=source)
-            nc.vector.quantize_mx(
-                out=w_codes[:, r, :].bitcast(FP8X4),
-                scales=w_scales[:, r, :],
-                in_=w_grouped[:].rearrange("p g n t -> p (g n t)"),
+        mem_k_sq = keep.tile([HEADS, MEM_SLOTS, FEATURES], F32)
+        mem_k_ss = keep.tile([HEADS, MEM_SLOTS], F32)
+        mem_k_rsqrt = keep.tile([HEADS, MEM_SLOTS], F32)
+        mem_k_factor = keep.tile([HEADS, MEM_SLOTS], F32)
+        mem_k_out = keep.tile([HEADS, MEM_SLOTS, FEATURES], F32)
+        mem_v_out = keep.tile([HEADS, MEM_SLOTS, FEATURES], F32)
+
+        def memory_values():
+            nc.gpsimd.tensor_scalar(
+                out=mem_v_out[:], in0=mem_v_raw[:], scalar1=1.0, scalar2=0.0, op0=ALU.mult, op1=ALU.add
             )
+            for b in range(BATCH):
+                nc.sync.dma_start(out=out_v[b, :, 0:MEM_SLOTS, :], in_=mem_v_out[:])
 
-        def project_and_rotate(w, part, token_tile, rows):
-            r = w * PARTS + part
-            b, j = divmod(token_tile, TILES_PER_BATCH)
-            acc = psum_acc.tile([P, BANK_COLUMNS], F32, name="acc")
-            for g in range(PASSES):
-                tokens = slice(j * P, (j + 1) * P)
-                columns = slice(g * BANK_COLUMNS, (g + 1) * BANK_COLUMNS)
-                nc.tensor.matmul_mx(
-                    out=acc[:],
-                    lhsT=x_codes[:, b, g, tokens].bitcast(FP8X4),
-                    lhsT_scale=x_scales[:, b, g, tokens],
-                    rhs=w_codes[:, r, columns].bitcast(FP8X4),
-                    rhs_scale=w_scales[:, r, columns],
-                    start=(g == 0),
-                    stop=(g == PASSES - 1),
-                )
-            squares = stage.tile([P, BANK_HEADS, FEATURES], F32)
-            sum_sq = norms.tile([P, BANK_HEADS], F32)
-            for h in range(BANK_HEADS):
-                nc.scalar.activation(
-                    out=squares[:, h, :],
-                    in_=acc[:, h * FEATURES : (h + 1) * FEATURES],
-                    func=ACT.Square,
-                    accum_out=sum_sq[:, h : h + 1],
-                )
-            above = norms.tile([P, BANK_HEADS], F32)
-            nc.scalar.activation(out=above[:], in_=sum_sq[:], func=ACT.Relu, bias=-EPS * EPS)
-            factor = norms.tile([P, BANK_HEADS], F32)
-            nc.scalar.activation(out=factor[:], in_=above[:], func=ACT.Abs_reciprocal_sqrt, bias=EPS * EPS)
-            shape = [P, BANK_HEADS, 2, FEATURES]
-            products = rotated.tile(shape, F32, name="products")
-            spread = acc[:].rearrange("p (h d) -> p h d", d=FEATURES).unsqueeze(2).to_broadcast(shape)
-            factors_of_tile = table[:, j].rearrange("p o a c -> p o (a c)")
-            for h in range(BANK_HEADS):
-                nc.vector.scalar_tensor_tensor(
-                    out=products[:, h],
-                    in0=spread[:, h],
-                    scalar=factor[:, h : h + 1],
-                    in1=factors_of_tile,
-                    op0=ALU.mult,
-                    op1=ALU.mult,
-                )
-            by_half = products[:].rearrange("p h o (a c) -> p h o a c", a=2)
-            nc.gpsimd.tensor_tensor(
-                out=rows.rearrange("p h (o c) -> p h o c", o=2),
-                in0=by_half[:, :, :, 0, :],
-                in1=by_half[:, :, :, 1, :],
-                op=ALU.add,
-            )
-
-        def memory_rows():
-            mem_k_sq = keep.tile([HEADS, MEM_SLOTS, FEATURES], F32)
+        def memory_key_squares():
             nc.scalar.activation(out=mem_k_sq[:], in_=mem_k_raw[:], func=ACT.Square)
-            mem_k_ss = keep.tile([HEADS, MEM_SLOTS], F32)
+
+        def memory_key_sums():
             nc.vector.tensor_reduce(out=mem_k_ss[:], in_=mem_k_sq[:], axis=mybir.AxisListType.X, op=ALU.add)
-            mem_k_rsqrt = keep.tile([HEADS, MEM_SLOTS], F32)
+
+        def memory_key_norms():
             nc.scalar.activation(out=mem_k_rsqrt[:], in_=mem_k_ss[:], func=ACT.Abs_reciprocal_sqrt)
-            mem_k_factor = keep.tile([HEADS, MEM_SLOTS], F32)
+
+        def memory_key_factors():
             nc.vector.tensor_scalar_min(out=mem_k_factor[:], in0=mem_k_rsqrt[:], scalar1=1.0 / EPS)
-            mem_k_out = keep.tile([HEADS, MEM_SLOTS, FEATURES], F32)
+
+        def memory_keys():
             nc.gpsimd.tensor_tensor(
                 out=mem_k_out[:],
                 in0=mem_k_raw[:],
                 in1=mem_k_factor[:].unsqueeze(2).to_broadcast([HEADS, MEM_SLOTS, FEATURES]),
                 op=ALU.mult,
             )
-            mem_v_out = keep.tile([HEADS, MEM_SLOTS, FEATURES], F32)
-            nc.gpsimd.tensor_scalar(
-                out=mem_v_out[:], in0=mem_v_raw[:], scalar1=1.0, scalar2=0.0, op0=ALU.mult, op1=ALU.add
-            )
             for b in range(BATCH):
-                nc.scalar.dma_start(out=out_k[b, :, 0:MEM_SLOTS, :], in_=mem_k_out[:])
-                nc.scalar.dma_start(out=out_v[b, :, 0:MEM_SLOTS, :], in_=mem_v_out[:])
+                nc.sync.dma_start(out=out_k[b, :, 0:MEM_SLOTS, :], in_=mem_k_out[:])
 
-        def store(w, part, b, first_tile, result):
-            heads = slice(part * BANK_HEADS, (part + 1) * BANK_HEADS)
-            positions = slice(first_position[w], first_position[w] + POSITIONS)
-            by_tile = outputs[w][b, heads, positions, :].rearrange("h (p j) d -> p h j d", j=TILES_PER_BATCH)
-            nc.sync.dma_start(out=by_tile[:, :, first_tile : first_tile + TILES_PER_STORE, :], in_=result[:])
+        every = slice(0, BANK_COLUMNS)
+        halves = [slice(0, BANK_COLUMNS // 2), slice(BANK_COLUMNS // 2, BANK_COLUMNS)]
+        memory_values()
+        for token_tile in range(TILES_PER_BATCH):
+            transpose_x_tile(token_tile)
+        for u in range(2):
+            turn_table(u)
+        quantise_x(0)
+        open_grouped(V, 0)
+        lay_by_vector(V, 0, every)
+        nc.vector.tensor_copy(out=turned_table[:, 1, :], in_=turned[1][:])
+        lay_by_scalar(V, 0, every)
+        nc.scalar.copy(out=turned_table[:, 0, :], in_=turned[0][:])
+        quantise_w(V, 0)
+        open_grouped(Q, 0)
+        lay_by_vector(Q, 0, every)
+        lay_by_scalar(Q, 0, every)
 
-        for arrival in arrivals:
-            if arrival[0] == "x":
-                quantise_x_tile(arrival[1])
-            else:
-                quantise_w_range(arrival[1], arrival[2])
-            if arrival == ("w", 2, 0):
-                turn_table()
+        items = [(V, unit) for unit in range(EARLY_V)]
+        for unit in range(UNITS):
+            items += [(Q, unit), (K, unit)]
+            if unit % 4 != 0:
+                items.append((V, EARLY_V + unit - unit // 4 - 1))
 
-        open_result = [None] * len(weights)
-        for w, unit in banks:
-            part, place_in_part = divmod(unit, TOKEN_TILES)
-            if w < 2:
-                b, j = divmod(place_in_part, TILES_PER_BATCH)
-                place = j % TILES_PER_STORE
-                if place == 0:
-                    open_result[w] = results.tile([P, BANK_HEADS, TILES_PER_STORE, FEATURES], F32, name="result%d" % w)
-                project_and_rotate(w, part, place_in_part, open_result[w][:, :, place, :])
-                if place == TILES_PER_STORE - 1:
-                    store(w, part, b, j - place, open_result[w])
-            else:
-                b, pair = divmod(place_in_part, PAIRS_PER_PART)
-                place = pair % PAIRS_PER_STORE
-                if place == 0:
-                    open_result[w] = results.tile([P, 2 * PAIRS_PER_STORE, TILES_PER_BATCH, FEATURES], F32, name="result2")
-                project_and_rotate_v(part, b, pair, open_result[w][:, 2 * place : 2 * place + 2])
-                if place == PAIRS_PER_STORE - 1:
-                    first_head = part * BANK_HEADS + 2 * (pair - place)
-                    rows_of_heads = out_v[b, first_head : first_head + 2 * PAIRS_PER_STORE, MEM_SLOTS : MEM_SLOTS + POSITIONS, :]
-                    nc.sync.dma_start(
-                        out=rows_of_heads.rearrange("h (p j) d -> p h (j d)", j=TILES_PER_BATCH),
-                        in_=open_result[w][:].rearrange("p h j d -> p h (j d)"),
-                    )
-            if (w, unit) == (len(weights) - 1, TOKEN_TILES // 2):
-                memory_rows()
+        before = {
+            2: [lambda: quantise_w(Q, 0), lambda: open_grouped(K, 0), lambda: lay_by_gpsimd(K, 0, every), lambda: lay_by_scalar(K, 0, every)],
+            3: [lambda: quantise_w(K, 0)],
+            6: [lambda: quantise_x(1)],
+            8: [lambda: open_grouped(V, 1), lambda: lay_by_gpsimd(V, 1, halves[0]), lambda: lay_by_scalar(V, 1, halves[0])],
+            9: [lambda: lay_by_gpsimd(V, 1, halves[1]), lambda: lay_by_scalar(V, 1, halves[1])],
+            13: [lambda: quantise_w(V, 1), lambda: open_grouped(Q, 1), lambda: lay_by_gpsimd(Q, 1, halves[0]), lambda: lay_by_scalar(Q, 1, halves[0])],
+            14: [lambda: lay_by_gpsimd(Q, 1, halves[1]), lambda: lay_by_scalar(Q, 1, halves[1])],
+            18: [lambda: quantise_w(Q, 1), lambda: open_grouped(K, 1), lambda: lay_by_gpsimd(K, 1, halves[0]), lambda: lay_by_scalar(K, 1, halves[0])],
+            19: [lambda: lay_by_gpsimd(K, 1, halves[1]), lambda: lay_by_scalar(K, 1, halves[1])],
+            22: [lambda: quantise_w(K, 1)],
+            26: [memory_key_squares],
+            28: [memory_key_sums],
+            29: [memory_key_norms],
+            31: [memory_key_factors],
+            32: [memory_keys],
+        }
+        behind = {0: lambda: [transpose_x_tile(t) for t in range(TILES_PER_BATCH, TOKEN_TILES)]}
+        quantised = {(V, 0): 0, (Q, 0): 2, (K, 0): 3, (V, 1): 13, (Q, 1): 18, (K, 1): 22}
+        batch_quantised = [0, 6]
+
+        def possible(item):
+            part, place_in_part = divmod(item[1], TOKEN_TILES)
+            return max(quantised[item[0], part], batch_quantised[place_in_part // TILES_PER_BATCH])
+
+        last = len(items) - 1
+        normed = [index for index in range(len(items)) if items[index][0] != V]
+        issued, summed, inverted = 0, 0, 0
+        for tick in range(len(items) + 2):
+            for step in before.get(tick, []):
+                step()
+            while issued <= min(last, tick + 5) and possible(items[issued]) <= tick:
+                matmuls(items[issued])
+                issued += 1
+            while summed < len(normed) and normed[summed] <= tick + 3 and normed[summed] < issued:
+                sum_squares(items[normed[summed]], range(0, BANK_HEADS // 2))
+                if inverted < summed:
+                    clip(items[normed[inverted]])
+                sum_squares(items[normed[summed]], range(BANK_HEADS // 2, BANK_HEADS))
+                if inverted < summed:
+                    invert(items[normed[inverted]])
+                    inverted += 1
+                summed += 1
+            if inverted < summed and normed[inverted] <= tick + 1:
+                clip(items[normed[inverted]])
+                invert(items[normed[inverted]])
+                inverted += 1
+            if tick >= 2 and items[tick - 2][0] == V:
+                copy_back(items[tick - 2])
+            if tick <= last:
+                multiply(items[tick])
+                if items[tick][0] != V:
+                    add(items[tick])
+            if 1 <= tick <= last + 1 and items[tick - 1][0] == V:
+                turn_back(items[tick - 1])
+            if tick in behind:
+                behind[tick]()

@@ -108,10 +108,10 @@ def tile_attention_pa_kernel(tc, x, freqs, Wq, Wk, Wv, mem_k, mem_v, out_q, out_
             nc.scalar.activation(out=target, in_=angles[:, :, 1, :], func=ACT.Sin)
         for target in (blocks[:, :, 3, :], table[:, :, 0, 1, :]):
             nc.scalar.activation(out=target, in_=angles[:, :, 0, :], func=ACT.Sin, scale=-1.0)
-        ones = keep.tile([P, 1], F32)
-        nc.vector.memset(ones[:], 1.0)
         inverse_of_one = keep.tile([P, 1], F32)
-        nc.scalar.activation(out=inverse_of_one[:], in_=ones[:], func=ACT.Abs_reciprocal_sqrt)
+        nc.scalar.activation(
+            out=inverse_of_one[:], in_=table[:, 0, 0, 1, 0:1], func=ACT.Abs_reciprocal_sqrt, scale=0.0, bias=1.0
+        )
         half_sin_sq = keep.tile([P, TILES_PER_BATCH, 2, HALF], F32)
         nc.vector.tensor_tensor(out=half_sin_sq[:], in0=half_sin[:], in1=half_sin[:], op=ALU.mult)
         for first in (0, 4):
@@ -136,7 +136,7 @@ def tile_attention_pa_kernel(tc, x, freqs, Wq, Wk, Wv, mem_k, mem_v, out_q, out_
             if j == 0:
                 x_grouped[b] = keep.tile([P, PASSES, POSITIONS * PACK], BF16, name="x_grouped%d" % b, align_bytes=64)
             words = x_raw[token_tile][:].bitcast(F32)
-            transposed = psum_aux.tile([P, PASSES * 2, P], F32, name="aux")
+            transposed = psum_acc.tile([P, PASSES * 2, P], F32, name="acc")
             for g in range(PASSES):
                 for u in range(2):
                     first_word = g * WORDS_PER_PASS + u
@@ -144,10 +144,12 @@ def tile_attention_pa_kernel(tc, x, freqs, Wq, Wk, Wv, mem_k, mem_v, out_q, out_
                         transposed[:, 2 * g + u, :], words[:, first_word : first_word + WORDS_PER_PASS - 1 : 2], identity[:]
                     )
             rows = x_grouped[b][:, :, j * P * PACK : (j + 1) * P * PACK]
-            nc.scalar.copy(
-                out=rows.bitcast(F32).rearrange("p g (r u) -> p g r u", u=2),
-                in_=transposed[:].rearrange("p (g u) r -> p g r u", g=PASSES),
-            )
+            target = rows.bitcast(F32).rearrange("p g (r u) -> p g r u", u=2)
+            source = transposed[:].rearrange("p (g u) r -> p g r u", g=PASSES)
+            if b == 0 and j % 2 == 1:
+                nc.vector.tensor_copy(out=target, in_=source)
+            else:
+                nc.scalar.copy(out=target, in_=source)
 
         def quantise_x(b):
             nc.vector.quantize_mx(
@@ -159,7 +161,7 @@ def tile_attention_pa_kernel(tc, x, freqs, Wq, Wk, Wv, mem_k, mem_v, out_q, out_
         turned = [None, None]
 
         def turn_table(u):
-            turned[u] = psum_aux.tile([P, POSITIONS], F32, name="aux")
+            turned[u] = psum_acc.tile([P, POSITIONS], F32, name="acc")
             for j in range(TILES_PER_BATCH):
                 nc.tensor.transpose(
                     turned[u][:, j * P : (j + 1) * P],

@@ -31,6 +31,9 @@ UNITS = PARTS * TOKEN_TILES
 PAIR = 2 * FEATURES
 PAIRS_PER_PART = BANK_COLUMNS // PAIR
 PAIRS_PER_STORE = 2
+MEM_GROUPS = 4
+MEM_ROWS = MEM_SLOTS // MEM_GROUPS
+GPSIMD_V = (9, 12)
 WORDS_PER_PASS = K_PASS // 2
 
 FLOPS = 2 * BATCH * POSITIONS * DIM * 3 * HEADS * FEATURES
@@ -53,10 +56,6 @@ def tile_attention_pa_kernel(tc, x, freqs, Wq, Wk, Wv, mem_k, mem_v, out_q, out_
 
         angles = keep.tile([P, TILES_PER_BATCH, 2, HALF], BF16)
         nc.scalar.dma_start(out=angles[:], in_=freqs.rearrange("(p j) (a c) -> p j a c", j=TILES_PER_BATCH, a=2))
-        mem_k_raw = keep.tile([HEADS, MEM_SLOTS, FEATURES], BF16)
-        nc.scalar.dma_start(out=mem_k_raw[:], in_=mem_k)
-        mem_v_raw = keep.tile([HEADS, MEM_SLOTS, FEATURES], BF16)
-        nc.scalar.dma_start(out=mem_v_raw[:], in_=mem_v)
 
         x_raw = [keep.tile([P, DIM], BF16, name="x_raw%d" % t) for t in range(TOKEN_TILES)]
         w_raw = [
@@ -87,6 +86,13 @@ def tile_attention_pa_kernel(tc, x, freqs, Wq, Wk, Wv, mem_k, mem_v, out_q, out_
             load_x(token_tile)
         for w in (V, Q, K):
             load_w(w, 1)
+        mem_k_raw = keep.tile([MEM_GROUPS * HEADS, MEM_ROWS, FEATURES], BF16)
+        mem_v_raw = keep.tile([MEM_GROUPS * HEADS, MEM_ROWS, FEATURES], BF16)
+        for group in range(MEM_GROUPS):
+            heads = slice(group * HEADS, (group + 1) * HEADS)
+            slots = slice(group * MEM_ROWS, (group + 1) * MEM_ROWS)
+            nc.sync.dma_start(out=mem_k_raw[heads], in_=mem_k[:, slots, :])
+            nc.sync.dma_start(out=mem_v_raw[heads], in_=mem_v[:, slots, :])
 
         identity = keep.tile([P, P], F32)
         make_identity(nc, identity[:])
@@ -169,42 +175,28 @@ def tile_attention_pa_kernel(tc, x, freqs, Wq, Wk, Wv, mem_k, mem_v, out_q, out_
                     identity[:],
                 )
 
-        def open_grouped(w, part):
-            by_scalar = stage.tile([P, BANK_COLUMNS, PACK], BF16, name="by_scalar", align_bytes=64)
-            by_other = keep.tile([P, BANK_COLUMNS, PACK], BF16, name="by_other", align_bytes=64)
-            w_grouped[w * PARTS + part] = [by_scalar, by_other]
-
-        def lay_by_scalar(w, part, columns):
-            nc.scalar.copy(
-                out=w_grouped[w * PARTS + part][0][:, columns].rearrange("p (c i) t -> p c t i", i=4),
-                in_=w_raw[w][part][:, 0, :, columns].rearrange("p t (c i) -> p c t i", i=4),
-            )
-
-        def lay_by_vector(w, part, columns):
+        def lay_by_vector(w, part, g):
             nc.vector.tensor_copy(
-                out=w_grouped[w * PARTS + part][1][:, columns].rearrange("p (c i) t -> p c t i", i=4),
-                in_=w_raw[w][part][:, 1, :, columns].rearrange("p t (c i) -> p c t i", i=4),
+                out=w_grouped[w * PARTS + part][:, g].rearrange("p (c i) t -> p c t i", i=4),
+                in_=w_raw[w][part][:, g].rearrange("p t (c i) -> p c t i", i=4),
             )
 
-        def lay_by_gpsimd(w, part, columns):
-            nc.gpsimd.tensor_scalar(
-                out=w_grouped[w * PARTS + part][1][:, columns],
-                in0=w_raw[w][part][:, 1, :, columns].rearrange("p t n -> p n t"),
-                scalar1=1.0,
-                scalar2=0.0,
-                op0=ALU.mult,
-                op1=ALU.add,
+        def lay_by_scalar(w, part, g):
+            nc.scalar.copy(
+                out=w_grouped[w * PARTS + part][:, g].rearrange("p (c i) t -> p c t i", i=4),
+                in_=w_raw[w][part][:, g].rearrange("p t (c i) -> p c t i", i=4),
             )
 
         def quantise_w(w, part):
             r = w * PARTS + part
-            for g in range(PASSES):
-                columns = slice(g * BANK_COLUMNS, (g + 1) * BANK_COLUMNS)
-                nc.vector.quantize_mx(
-                    out=w_codes[:, r, columns].bitcast(FP8X4),
-                    scales=w_scales[:, r, columns],
-                    in_=w_grouped[r][g][:].rearrange("p n t -> p (n t)"),
-                )
+            w_grouped[r] = stage.tile([P, PASSES, BANK_COLUMNS, PACK], BF16, name="w_grouped", align_bytes=64)
+            lay_by_scalar(w, part, 0)
+            lay_by_vector(w, part, 1)
+            nc.vector.quantize_mx(
+                out=w_codes[:, r, :].bitcast(FP8X4),
+                scales=w_scales[:, r, :],
+                in_=w_grouped[r][:].rearrange("p g n t -> p (g n t)"),
+            )
 
         state = {}
         open_result = [None] * len(weights)
@@ -265,9 +257,13 @@ def tile_attention_pa_kernel(tc, x, freqs, Wq, Wk, Wv, mem_k, mem_v, out_q, out_
             state[item]["products"] = products
             if w == V:
                 shape = [P, 2, POSITIONS]
-                nc.vector.tensor_tensor(
+                engine, values = nc.vector, acc
+                if unit in GPSIMD_V:
+                    engine, values = nc.gpsimd, stage.tile([P, POSITIONS], F32, name="values")
+                    nc.scalar.copy(out=values[:], in_=acc[:])
+                engine.tensor_tensor(
                     out=products[:].rearrange("p (u n) -> p u n", u=2),
-                    in0=acc[:].unsqueeze(1).to_broadcast(shape),
+                    in0=values[:].unsqueeze(1).to_broadcast(shape),
                     in1=turned_table[:],
                     op=ALU.mult,
                 )
@@ -338,98 +334,59 @@ def tile_attention_pa_kernel(tc, x, freqs, Wq, Wk, Wv, mem_k, mem_v, out_q, out_
                     in_=open_result[w][:].rearrange("p h j d -> p h (j d)"),
                 )
 
-        mem_k_sq = keep.tile([HEADS, MEM_SLOTS, FEATURES], F32)
-        mem_k_ss = keep.tile([HEADS, MEM_SLOTS], F32)
-        mem_k_rsqrt = keep.tile([HEADS, MEM_SLOTS], F32)
-        mem_k_factor = keep.tile([HEADS, MEM_SLOTS], F32)
-        mem_k_out = keep.tile([HEADS, MEM_SLOTS, FEATURES], F32)
-        mem_v_out = keep.tile([HEADS, MEM_SLOTS, FEATURES], F32)
-
-        def memory_values():
+        def memory_rows():
+            shape = [MEM_GROUPS * HEADS, MEM_ROWS, FEATURES]
+            mem_k_sq = keep.tile(shape, F32)
+            nc.scalar.activation(out=mem_k_sq[:], in_=mem_k_raw[:], func=ACT.Square)
+            mem_k_ss = keep.tile(shape[:2], F32)
+            nc.vector.tensor_reduce(out=mem_k_ss[:], in_=mem_k_sq[:], axis=mybir.AxisListType.X, op=ALU.add)
+            mem_k_rsqrt = keep.tile(shape[:2], F32)
+            nc.scalar.activation(out=mem_k_rsqrt[:], in_=mem_k_ss[:], func=ACT.Abs_reciprocal_sqrt)
+            mem_k_factor = keep.tile(shape[:2], F32)
+            nc.vector.tensor_scalar_min(out=mem_k_factor[:], in0=mem_k_rsqrt[:], scalar1=1.0 / EPS)
+            mem_k_out = keep.tile(shape, F32)
+            nc.gpsimd.tensor_tensor(
+                out=mem_k_out[:], in0=mem_k_raw[:], in1=mem_k_factor[:].unsqueeze(2).to_broadcast(shape), op=ALU.mult
+            )
+            mem_v_out = keep.tile(shape, F32)
             nc.gpsimd.tensor_scalar(
                 out=mem_v_out[:], in0=mem_v_raw[:], scalar1=1.0, scalar2=0.0, op0=ALU.mult, op1=ALU.add
             )
             for b in range(BATCH):
-                nc.sync.dma_start(out=out_v[b, :, 0:MEM_SLOTS, :], in_=mem_v_out[:])
+                for group in range(MEM_GROUPS):
+                    heads = slice(group * HEADS, (group + 1) * HEADS)
+                    slots = slice(group * MEM_ROWS, (group + 1) * MEM_ROWS)
+                    nc.sync.dma_start(out=out_k[b, :, slots, :], in_=mem_k_out[heads])
+                    nc.sync.dma_start(out=out_v[b, :, slots, :], in_=mem_v_out[heads])
 
-        def memory_key_squares():
-            nc.scalar.activation(out=mem_k_sq[:], in_=mem_k_raw[:], func=ACT.Square)
-
-        def memory_key_sums():
-            nc.vector.tensor_reduce(out=mem_k_ss[:], in_=mem_k_sq[:], axis=mybir.AxisListType.X, op=ALU.add)
-
-        def memory_key_norms():
-            nc.scalar.activation(out=mem_k_rsqrt[:], in_=mem_k_ss[:], func=ACT.Abs_reciprocal_sqrt)
-
-        def memory_key_factors():
-            nc.vector.tensor_scalar_min(out=mem_k_factor[:], in0=mem_k_rsqrt[:], scalar1=1.0 / EPS)
-
-        def memory_keys():
-            nc.gpsimd.tensor_tensor(
-                out=mem_k_out[:],
-                in0=mem_k_raw[:],
-                in1=mem_k_factor[:].unsqueeze(2).to_broadcast([HEADS, MEM_SLOTS, FEATURES]),
-                op=ALU.mult,
-            )
-            for b in range(BATCH):
-                nc.sync.dma_start(out=out_k[b, :, 0:MEM_SLOTS, :], in_=mem_k_out[:])
-
-        every = slice(0, BANK_COLUMNS)
-        halves = [slice(0, BANK_COLUMNS // 2), slice(BANK_COLUMNS // 2, BANK_COLUMNS)]
-        memory_values()
         for token_tile in range(TILES_PER_BATCH):
             transpose_x_tile(token_tile)
         for u in range(2):
             turn_table(u)
         quantise_x(0)
-        open_grouped(V, 0)
-        lay_by_vector(V, 0, every)
-        nc.vector.tensor_copy(out=turned_table[:, 1, :], in_=turned[1][:])
-        lay_by_scalar(V, 0, every)
-        nc.scalar.copy(out=turned_table[:, 0, :], in_=turned[0][:])
         quantise_w(V, 0)
-        open_grouped(Q, 0)
-        lay_by_vector(Q, 0, every)
-        lay_by_scalar(Q, 0, every)
+        nc.vector.tensor_copy(out=turned_table[:, 1, :], in_=turned[1][:])
+        nc.scalar.copy(out=turned_table[:, 0, :], in_=turned[0][:])
+        quantise_w(Q, 0)
+        for token_tile in range(TILES_PER_BATCH, TOKEN_TILES):
+            transpose_x_tile(token_tile)
+        quantise_x(1)
+        quantise_w(K, 0)
+        for w in (V, Q, K):
+            quantise_w(w, 1)
+        memory_rows()
 
         items = [(V, unit) for unit in range(EARLY_V)]
         for unit in range(UNITS):
             items += [(Q, unit), (K, unit)]
-            if unit % 4 != 0:
-                items.append((V, EARLY_V + unit - unit // 4 - 1))
-
-        before = {
-            2: [lambda: quantise_w(Q, 0), lambda: open_grouped(K, 0), lambda: lay_by_gpsimd(K, 0, every), lambda: lay_by_scalar(K, 0, every)],
-            3: [lambda: quantise_w(K, 0)],
-            6: [lambda: quantise_x(1)],
-            8: [lambda: open_grouped(V, 1), lambda: lay_by_gpsimd(V, 1, halves[0]), lambda: lay_by_scalar(V, 1, halves[0])],
-            9: [lambda: lay_by_gpsimd(V, 1, halves[1]), lambda: lay_by_scalar(V, 1, halves[1])],
-            13: [lambda: quantise_w(V, 1), lambda: open_grouped(Q, 1), lambda: lay_by_gpsimd(Q, 1, halves[0]), lambda: lay_by_scalar(Q, 1, halves[0])],
-            14: [lambda: lay_by_gpsimd(Q, 1, halves[1]), lambda: lay_by_scalar(Q, 1, halves[1])],
-            18: [lambda: quantise_w(Q, 1), lambda: open_grouped(K, 1), lambda: lay_by_gpsimd(K, 1, halves[0]), lambda: lay_by_scalar(K, 1, halves[0])],
-            19: [lambda: lay_by_gpsimd(K, 1, halves[1]), lambda: lay_by_scalar(K, 1, halves[1])],
-            22: [lambda: quantise_w(K, 1)],
-            26: [memory_key_squares],
-            28: [memory_key_sums],
-            29: [memory_key_norms],
-            31: [memory_key_factors],
-            32: [memory_keys],
-        }
-        behind = {0: lambda: [transpose_x_tile(t) for t in range(TILES_PER_BATCH, TOKEN_TILES)]}
-        quantised = {(V, 0): 0, (Q, 0): 2, (K, 0): 3, (V, 1): 13, (Q, 1): 18, (K, 1): 22}
-        batch_quantised = [0, 6]
-
-        def possible(item):
-            part, place_in_part = divmod(item[1], TOKEN_TILES)
-            return max(quantised[item[0], part], batch_quantised[place_in_part // TILES_PER_BATCH])
+            if unit % 4 != 3:
+                items.append((V, EARLY_V + unit - unit // 4))
 
         last = len(items) - 1
         normed = [index for index in range(len(items)) if items[index][0] != V]
         issued, summed, inverted = 0, 0, 0
         for tick in range(len(items) + 2):
-            for step in before.get(tick, []):
-                step()
-            while issued <= min(last, tick + 5) and possible(items[issued]) <= tick:
+            while issued <= min(last, tick + 5):
                 matmuls(items[issued])
                 issued += 1
             while summed < len(normed) and normed[summed] <= tick + 3 and normed[summed] < issued:
@@ -453,5 +410,3 @@ def tile_attention_pa_kernel(tc, x, freqs, Wq, Wk, Wv, mem_k, mem_v, out_q, out_
                     add(items[tick])
             if 1 <= tick <= last + 1 and items[tick - 1][0] == V:
                 turn_back(items[tick - 1])
-            if tick in behind:
-                behind[tick]()

@@ -20,7 +20,7 @@ PACK = 4
 K_PASS = P * PACK
 PASSES = DIM // K_PASS
 Q, K, V = 0, 1, 2
-EARLY_V = 4
+EARLY_V = 8
 TILES_PER_BATCH = POSITIONS // P
 TOKEN_TILES = BATCH * TILES_PER_BATCH
 TILES_PER_STORE = 2
@@ -33,7 +33,7 @@ PAIRS_PER_PART = BANK_COLUMNS // PAIR
 PAIRS_PER_STORE = 2
 MEM_GROUPS = 4
 MEM_ROWS = MEM_SLOTS // MEM_GROUPS
-GPSIMD_V = (9, 12)
+GPSIMD_V = ()
 WORDS_PER_PASS = K_PASS // 2
 
 FLOPS = 2 * BATCH * POSITIONS * DIM * 3 * HEADS * FEATURES
@@ -94,6 +94,8 @@ def tile_attention_pa_kernel(tc, x, freqs, Wq, Wk, Wv, mem_k, mem_v, out_q, out_
             nc.sync.dma_start(out=mem_k_raw[heads], in_=mem_k[:, slots, :])
             nc.sync.dma_start(out=mem_v_raw[heads], in_=mem_v[:, slots, :])
 
+        ctx.enter_context(tc.manual_schedule(engines={mybir.EngineType.DVE, mybir.EngineType.Pool}))
+
         identity = keep.tile([P, P], F32)
         make_identity(nc, identity[:])
         moves = keep.tile([P, 2, 2, FEATURES], F32)
@@ -135,7 +137,7 @@ def tile_attention_pa_kernel(tc, x, freqs, Wq, Wk, Wv, mem_k, mem_v, out_q, out_
         w_codes = keep.tile([P, len(weights) * PARTS, PASSES * BANK_COLUMNS], U32, align_bytes=64)
         w_scales = keep.tile([P, len(weights) * PARTS, PASSES * BANK_COLUMNS], U8, align_bytes=64)
         x_grouped = [None] * BATCH
-        w_grouped = [None] * (len(weights) * PARTS)
+        w_grouped = [[None, None] for r in range(len(weights) * PARTS)]
 
         def transpose_x_tile(token_tile):
             b, j = divmod(token_tile, TILES_PER_BATCH)
@@ -152,7 +154,7 @@ def tile_attention_pa_kernel(tc, x, freqs, Wq, Wk, Wv, mem_k, mem_v, out_q, out_
             rows = x_grouped[b][:, :, j * P * PACK : (j + 1) * P * PACK]
             target = rows.bitcast(F32).rearrange("p g (r u) -> p g r u", u=2)
             source = transposed[:].rearrange("p (g u) r -> p g r u", g=PASSES)
-            if b == 0 and j % 2 == 1:
+            if b == 0:
                 nc.vector.tensor_copy(out=target, in_=source)
             else:
                 nc.scalar.copy(out=target, in_=source)
@@ -175,28 +177,43 @@ def tile_attention_pa_kernel(tc, x, freqs, Wq, Wk, Wv, mem_k, mem_v, out_q, out_
                     identity[:],
                 )
 
-        def lay_by_vector(w, part, g):
-            nc.vector.tensor_copy(
-                out=w_grouped[w * PARTS + part][:, g].rearrange("p (c i) t -> p c t i", i=4),
-                in_=w_raw[w][part][:, g].rearrange("p t (c i) -> p c t i", i=4),
+        def lay_by_scalar(w, part):
+            grouped = stage.tile([P, BANK_COLUMNS, PACK], BF16, name="by_scalar", align_bytes=64)
+            w_grouped[w * PARTS + part][0] = grouped
+            nc.scalar.copy(
+                out=grouped[:].rearrange("p (c i) t -> p c t i", i=4),
+                in_=w_raw[w][part][:, 0].rearrange("p t (c i) -> p c t i", i=4),
             )
 
-        def lay_by_scalar(w, part, g):
-            nc.scalar.copy(
-                out=w_grouped[w * PARTS + part][:, g].rearrange("p (c i) t -> p c t i", i=4),
-                in_=w_raw[w][part][:, g].rearrange("p t (c i) -> p c t i", i=4),
+        def lay_by_vector(w, part):
+            grouped = keep.tile([P, BANK_COLUMNS, PACK], BF16, name="by_other", align_bytes=64)
+            w_grouped[w * PARTS + part][1] = grouped
+            nc.vector.tensor_copy(
+                out=grouped[:].rearrange("p (c i) t -> p c t i", i=4),
+                in_=w_raw[w][part][:, 1].rearrange("p t (c i) -> p c t i", i=4),
+            )
+
+        def lay_by_gpsimd(w, part):
+            grouped = keep.tile([P, BANK_COLUMNS, PACK], BF16, name="by_other", align_bytes=64)
+            w_grouped[w * PARTS + part][1] = grouped
+            nc.gpsimd.tensor_scalar(
+                out=grouped[:],
+                in0=w_raw[w][part][:, 1].rearrange("p t n -> p n t"),
+                scalar1=1.0,
+                scalar2=0.0,
+                op0=ALU.mult,
+                op1=ALU.add,
             )
 
         def quantise_w(w, part):
             r = w * PARTS + part
-            w_grouped[r] = stage.tile([P, PASSES, BANK_COLUMNS, PACK], BF16, name="w_grouped", align_bytes=64)
-            lay_by_scalar(w, part, 0)
-            lay_by_vector(w, part, 1)
-            nc.vector.quantize_mx(
-                out=w_codes[:, r, :].bitcast(FP8X4),
-                scales=w_scales[:, r, :],
-                in_=w_grouped[r][:].rearrange("p g n t -> p (g n t)"),
-            )
+            for g in range(PASSES):
+                columns = slice(g * BANK_COLUMNS, (g + 1) * BANK_COLUMNS)
+                nc.vector.quantize_mx(
+                    out=w_codes[:, r, columns].bitcast(FP8X4),
+                    scales=w_scales[:, r, columns],
+                    in_=w_grouped[r][g][:].rearrange("p n t -> p (n t)"),
+                )
 
         state = {}
         open_result = [None] * len(weights)
@@ -334,21 +351,26 @@ def tile_attention_pa_kernel(tc, x, freqs, Wq, Wk, Wv, mem_k, mem_v, out_q, out_
                     in_=open_result[w][:].rearrange("p h j d -> p h (j d)"),
                 )
 
-        def memory_rows():
-            shape = [MEM_GROUPS * HEADS, MEM_ROWS, FEATURES]
-            mem_k_sq = keep.tile(shape, F32)
+        mem_shape = [MEM_GROUPS * HEADS, MEM_ROWS, FEATURES]
+        mem_k_sq = keep.tile(mem_shape, F32)
+        mem_k_ss = keep.tile(mem_shape[:2], F32)
+        mem_k_rsqrt = keep.tile(mem_shape[:2], F32)
+        mem_k_factor = keep.tile(mem_shape[:2], F32)
+        mem_k_out = keep.tile(mem_shape, F32)
+        mem_v_out = keep.tile(mem_shape, F32)
+
+        def memory_sums():
             nc.scalar.activation(out=mem_k_sq[:], in_=mem_k_raw[:], func=ACT.Square)
-            mem_k_ss = keep.tile(shape[:2], F32)
             nc.vector.tensor_reduce(out=mem_k_ss[:], in_=mem_k_sq[:], axis=mybir.AxisListType.X, op=ALU.add)
-            mem_k_rsqrt = keep.tile(shape[:2], F32)
+
+        def memory_factors():
             nc.scalar.activation(out=mem_k_rsqrt[:], in_=mem_k_ss[:], func=ACT.Abs_reciprocal_sqrt)
-            mem_k_factor = keep.tile(shape[:2], F32)
             nc.vector.tensor_scalar_min(out=mem_k_factor[:], in0=mem_k_rsqrt[:], scalar1=1.0 / EPS)
-            mem_k_out = keep.tile(shape, F32)
+
+        def memory_rows():
             nc.gpsimd.tensor_tensor(
-                out=mem_k_out[:], in0=mem_k_raw[:], in1=mem_k_factor[:].unsqueeze(2).to_broadcast(shape), op=ALU.mult
+                out=mem_k_out[:], in0=mem_k_raw[:], in1=mem_k_factor[:].unsqueeze(2).to_broadcast(mem_shape), op=ALU.mult
             )
-            mem_v_out = keep.tile(shape, F32)
             nc.gpsimd.tensor_scalar(
                 out=mem_v_out[:], in0=mem_v_raw[:], scalar1=1.0, scalar2=0.0, op0=ALU.mult, op1=ALU.add
             )
@@ -363,30 +385,52 @@ def tile_attention_pa_kernel(tc, x, freqs, Wq, Wk, Wv, mem_k, mem_v, out_q, out_
             transpose_x_tile(token_tile)
         for u in range(2):
             turn_table(u)
-        quantise_x(0)
-        quantise_w(V, 0)
-        nc.vector.tensor_copy(out=turned_table[:, 1, :], in_=turned[1][:])
+        lay_by_scalar(V, 0)
         nc.scalar.copy(out=turned_table[:, 0, :], in_=turned[0][:])
-        quantise_w(Q, 0)
-        for token_tile in range(TILES_PER_BATCH, TOKEN_TILES):
-            transpose_x_tile(token_tile)
-        quantise_x(1)
-        quantise_w(K, 0)
-        for w in (V, Q, K):
-            quantise_w(w, 1)
-        memory_rows()
+        quantise_x(0)
+        lay_by_vector(V, 0)
+        nc.vector.tensor_copy(out=turned_table[:, 1, :], in_=turned[1][:])
+        quantise_w(V, 0)
+        for w in (Q, K):
+            lay_by_scalar(w, 0)
+        lay_by_gpsimd(Q, 0)
 
         items = [(V, unit) for unit in range(EARLY_V)]
         for unit in range(UNITS):
             items += [(Q, unit), (K, unit)]
-            if unit % 4 != 3:
-                items.append((V, EARLY_V + unit - unit // 4))
+            if unit % 2 == 1:
+                items.append((V, EARLY_V + unit // 2))
+
+        def second_batch():
+            for token_tile in range(TILES_PER_BATCH, TOKEN_TILES):
+                transpose_x_tile(token_tile)
+
+        before = {
+            1: [lambda: quantise_w(Q, 0), lambda: lay_by_gpsimd(K, 0)],
+            2: [second_batch],
+            3: [lambda: quantise_w(K, 0), lambda: lay_by_gpsimd(V, 1), lambda: lay_by_scalar(V, 1)],
+            4: [lambda: quantise_x(1), lambda: quantise_w(V, 1), lambda: lay_by_gpsimd(Q, 1)],
+            5: [lambda: lay_by_scalar(Q, 1)],
+            6: [lambda: quantise_w(Q, 1), lambda: lay_by_gpsimd(K, 1), lambda: lay_by_scalar(K, 1)],
+            8: [lambda: quantise_w(K, 1)],
+            12: [memory_sums],
+            15: [memory_factors],
+            16: [memory_rows],
+        }
+        quantised = {(V, 0): 0, (Q, 0): 1, (K, 0): 3, (V, 1): 4, (Q, 1): 6, (K, 1): 8}
+        batch_quantised = [0, 4]
+
+        def possible(item):
+            part, place_in_part = divmod(item[1], TOKEN_TILES)
+            return max(quantised[item[0], part], batch_quantised[place_in_part // TILES_PER_BATCH])
 
         last = len(items) - 1
         normed = [index for index in range(len(items)) if items[index][0] != V]
         issued, summed, inverted = 0, 0, 0
         for tick in range(len(items) + 2):
-            while issued <= min(last, tick + 5):
+            for step in before.get(tick, []):
+                step()
+            while issued <= min(last, tick + 5) and possible(items[issued]) <= tick:
                 matmuls(items[issued])
                 issued += 1
             while summed < len(normed) and normed[summed] <= tick + 3 and normed[summed] < issued:

@@ -51,8 +51,8 @@ def tile_attention_pa_kernel(tc, x, freqs, Wq, Wk, Wv, mem_k, mem_v, out_q, out_
         norms = ctx.enter_context(tc.tile_pool(name="norms", bufs=8))
         rotated = ctx.enter_context(tc.tile_pool(name="rotated", bufs=8))
         results = ctx.enter_context(tc.tile_pool(name="results", bufs=3))
-        psum_aux = ctx.enter_context(tc.psum_pool(name="psum_aux", bufs=2))
-        psum_acc = ctx.enter_context(tc.psum_pool(name="psum_acc", bufs=6))
+        psum_aux = ctx.enter_context(tc.psum_pool(name="psum_aux", bufs=3))
+        psum_acc = ctx.enter_context(tc.psum_pool(name="psum_acc", bufs=5))
 
         angles = keep.tile([P, TILES_PER_BATCH, 2, HALF], BF16)
         nc.scalar.dma_start(out=angles[:], in_=freqs.rearrange("(p j) (a c) -> p j a c", j=TILES_PER_BATCH, a=2))
@@ -393,7 +393,9 @@ def tile_attention_pa_kernel(tc, x, freqs, Wq, Wk, Wv, mem_k, mem_v, out_q, out_
         quantise_w(V, 0)
         for w in (Q, K):
             lay_by_scalar(w, 0)
-        lay_by_gpsimd(Q, 0)
+        lay_by_vector(Q, 0)
+        quantise_w(Q, 0)
+        lay_by_gpsimd(K, 0)
 
         items = [(V, unit) for unit in range(EARLY_V)]
         for unit in range(UNITS):
@@ -406,9 +408,8 @@ def tile_attention_pa_kernel(tc, x, freqs, Wq, Wk, Wv, mem_k, mem_v, out_q, out_
                 transpose_x_tile(token_tile)
 
         before = {
-            1: [lambda: quantise_w(Q, 0), lambda: lay_by_gpsimd(K, 0)],
-            2: [second_batch],
-            3: [lambda: quantise_w(K, 0), lambda: lay_by_gpsimd(V, 1), lambda: lay_by_scalar(V, 1)],
+            1: [second_batch],
+            2: [lambda: quantise_w(K, 0), lambda: lay_by_gpsimd(V, 1), lambda: lay_by_scalar(V, 1)],
             4: [lambda: quantise_x(1), lambda: quantise_w(V, 1), lambda: lay_by_gpsimd(Q, 1)],
             5: [lambda: lay_by_scalar(Q, 1)],
             6: [lambda: quantise_w(Q, 1), lambda: lay_by_gpsimd(K, 1), lambda: lay_by_scalar(K, 1)],
@@ -417,7 +418,7 @@ def tile_attention_pa_kernel(tc, x, freqs, Wq, Wk, Wv, mem_k, mem_v, out_q, out_
             15: [memory_factors],
             16: [memory_rows],
         }
-        quantised = {(V, 0): 0, (Q, 0): 1, (K, 0): 3, (V, 1): 4, (Q, 1): 6, (K, 1): 8}
+        quantised = {(V, 0): 0, (Q, 0): 0, (K, 0): 2, (V, 1): 4, (Q, 1): 6, (K, 1): 8}
         batch_quantised = [0, 4]
 
         def possible(item):
@@ -430,7 +431,7 @@ def tile_attention_pa_kernel(tc, x, freqs, Wq, Wk, Wv, mem_k, mem_v, out_q, out_
         for tick in range(len(items) + 2):
             for step in before.get(tick, []):
                 step()
-            while issued <= min(last, tick + 5) and possible(items[issued]) <= tick:
+            while issued <= min(last, tick + (5 if tick else 1)) and possible(items[issued]) <= tick:
                 matmuls(items[issued])
                 issued += 1
             while summed < len(normed) and normed[summed] <= tick + 3 and normed[summed] < issued:

@@ -30,7 +30,7 @@ PARTS = HEADS // BANK_HEADS
 UNITS = PARTS * TOKEN_TILES
 PAIR = 2 * FEATURES
 PAIRS_PER_PART = BANK_COLUMNS // PAIR
-PAIRS_PER_STORE = 2
+PAIRS_PER_STORE = 1
 MEM_GROUPS = 4
 MEM_ROWS = MEM_SLOTS // MEM_GROUPS
 GPSIMD_V = ()
@@ -109,27 +109,30 @@ def tile_attention_pa_kernel(tc, x, freqs, Wq, Wk, Wv, mem_k, mem_v, out_q, out_
                 )
 
         half_sin = keep.tile([P, TILES_PER_BATCH, 2, HALF], F32)
-        nc.scalar.activation(out=half_sin[:], in_=angles[:], func=ACT.Sin, scale=0.5)
+        half_sin_sq = keep.tile([P, TILES_PER_BATCH, 2, HALF], F32)
         table = keep.tile([P, TILES_PER_BATCH, 2, 2, HALF], F32)
         blocks = keep.tile([P, TILES_PER_BATCH, 6, HALF], F32)
-        for target in (blocks[:, :, 2, :], table[:, :, 1, 0, :]):
-            nc.scalar.activation(out=target, in_=angles[:, :, 1, :], func=ACT.Sin)
-        for target in (blocks[:, :, 3, :], table[:, :, 0, 1, :]):
-            nc.scalar.activation(out=target, in_=angles[:, :, 0, :], func=ACT.Sin, scale=-1.0)
         inverse_of_one = keep.tile([P, 1], F32)
-        nc.scalar.activation(
-            out=inverse_of_one[:], in_=table[:, 0, 0, 1, 0:1], func=ACT.Abs_reciprocal_sqrt, scale=0.0, bias=1.0
-        )
-        half_sin_sq = keep.tile([P, TILES_PER_BATCH, 2, HALF], F32)
-        nc.vector.tensor_tensor(out=half_sin_sq[:], in0=half_sin[:], in1=half_sin[:], op=ALU.mult)
-        for first in (0, 4):
-            nc.vector.tensor_scalar(
-                out=blocks[:, :, first : first + 2, :], in0=half_sin_sq[:], scalar1=-2.0, scalar2=1.0, op0=ALU.mult, op1=ALU.add
+
+        def build_tables():
+            nc.scalar.activation(out=half_sin[:], in_=angles[:], func=ACT.Sin, scale=0.5)
+            for target in (blocks[:, :, 2, :], table[:, :, 1, 0, :]):
+                nc.scalar.activation(out=target, in_=angles[:, :, 1, :], func=ACT.Sin)
+            for target in (blocks[:, :, 3, :], table[:, :, 0, 1, :]):
+                nc.scalar.activation(out=target, in_=angles[:, :, 0, :], func=ACT.Sin, scale=-1.0)
+            nc.scalar.activation(
+                out=inverse_of_one[:], in_=table[:, 0, 0, 1, 0:1], func=ACT.Abs_reciprocal_sqrt, scale=0.0, bias=1.0
             )
-        for a in range(2):
-            nc.vector.tensor_scalar(
-                out=table[:, :, a, a, :], in0=half_sin_sq[:, :, a, :], scalar1=-2.0, scalar2=1.0, op0=ALU.mult, op1=ALU.add
-            )
+            nc.vector.tensor_tensor(out=half_sin_sq[:], in0=half_sin[:], in1=half_sin[:], op=ALU.mult)
+            for first in (0, 4):
+                nc.vector.tensor_scalar(
+                    out=blocks[:, :, first : first + 2, :], in0=half_sin_sq[:], scalar1=-2.0, scalar2=1.0, op0=ALU.mult, op1=ALU.add
+                )
+            for a in range(2):
+                nc.gpsimd.tensor_scalar(
+                    out=table[:, :, a, a, :], in0=half_sin_sq[:, :, a, :], scalar1=-2.0, scalar2=1.0, op0=ALU.mult, op1=ALU.add
+                )
+
         turned_table = keep.tile([P, 2, POSITIONS], F32)
 
         x_codes = keep.tile([P, BATCH, PASSES * POSITIONS], U32, align_bytes=64)
@@ -154,7 +157,7 @@ def tile_attention_pa_kernel(tc, x, freqs, Wq, Wk, Wv, mem_k, mem_v, out_q, out_
             rows = x_grouped[b][:, :, j * P * PACK : (j + 1) * P * PACK]
             target = rows.bitcast(F32).rearrange("p g (r u) -> p g r u", u=2)
             source = transposed[:].rearrange("p (g u) r -> p g r u", g=PASSES)
-            if b == 0:
+            if b == 0 and j >= 2:
                 nc.vector.tensor_copy(out=target, in_=source)
             else:
                 nc.scalar.copy(out=target, in_=source)
@@ -185,8 +188,8 @@ def tile_attention_pa_kernel(tc, x, freqs, Wq, Wk, Wv, mem_k, mem_v, out_q, out_
                 in_=w_raw[w][part][:, 0].rearrange("p t (c i) -> p c t i", i=4),
             )
 
-        def lay_by_vector(w, part):
-            grouped = keep.tile([P, BANK_COLUMNS, PACK], BF16, name="by_other", align_bytes=64)
+        def lay_by_vector(w, part, name):
+            grouped = keep.tile([P, BANK_COLUMNS, PACK], BF16, name=name, align_bytes=64)
             w_grouped[w * PARTS + part][1] = grouped
             nc.vector.tensor_copy(
                 out=grouped[:].rearrange("p (c i) t -> p c t i", i=4),
@@ -381,21 +384,24 @@ def tile_attention_pa_kernel(tc, x, freqs, Wq, Wk, Wv, mem_k, mem_v, out_q, out_
                     nc.sync.dma_start(out=out_k[b, :, slots, :], in_=mem_k_out[heads])
                     nc.sync.dma_start(out=out_v[b, :, slots, :], in_=mem_v_out[heads])
 
-        for token_tile in range(TILES_PER_BATCH):
-            transpose_x_tile(token_tile)
-        for u in range(2):
-            turn_table(u)
-        lay_by_scalar(V, 0)
-        nc.scalar.copy(out=turned_table[:, 0, :], in_=turned[0][:])
-        quantise_x(0)
-        lay_by_vector(V, 0)
-        nc.vector.tensor_copy(out=turned_table[:, 1, :], in_=turned[1][:])
-        quantise_w(V, 0)
-        for w in (Q, K):
-            lay_by_scalar(w, 0)
-        lay_by_vector(Q, 0)
-        quantise_w(Q, 0)
-        lay_by_gpsimd(K, 0)
+        pinned = {mybir.EngineType.DVE, mybir.EngineType.Pool, mybir.EngineType.Activation}
+        with tc.manual_schedule(engines=pinned):
+            build_tables()
+            for token_tile in range(TILES_PER_BATCH):
+                transpose_x_tile(token_tile)
+            for u in range(2):
+                turn_table(u)
+            lay_by_scalar(V, 0)
+            for u in range(2):
+                nc.scalar.copy(out=turned_table[:, u, :], in_=turned[u][:])
+            quantise_x(0)
+            lay_by_vector(V, 0, "by_vector")
+            lay_by_vector(Q, 0, "by_other")
+            quantise_w(V, 0)
+            for w in (Q, K):
+                lay_by_scalar(w, 0)
+            quantise_w(Q, 0)
+            lay_by_gpsimd(K, 0)
 
         items = [(V, unit) for unit in range(EARLY_V)]
         for unit in range(UNITS):

@@ -20,7 +20,8 @@ PACK = 4
 K_PASS = P * PACK
 PASSES = DIM // K_PASS
 Q, K, V = 0, 1, 2
-EARLY_V = 8
+LATE_V = (2, 4, 7, 10, 12, 15)
+EARLY_V = 10
 TILES_PER_BATCH = POSITIONS // P
 TOKEN_TILES = BATCH * TILES_PER_BATCH
 TILES_PER_STORE = 2
@@ -406,8 +407,8 @@ def tile_attention_pa_kernel(tc, x, freqs, Wq, Wk, Wv, mem_k, mem_v, out_q, out_
         items = [(V, unit) for unit in range(EARLY_V)]
         for unit in range(UNITS):
             items += [(Q, unit), (K, unit)]
-            if unit % 2 == 1:
-                items.append((V, EARLY_V + unit // 2))
+            if unit in LATE_V:
+                items.append((V, EARLY_V + LATE_V.index(unit)))
 
         def second_batch():
             for token_tile in range(TILES_PER_BATCH, TOKEN_TILES):
@@ -418,13 +419,13 @@ def tile_attention_pa_kernel(tc, x, freqs, Wq, Wk, Wv, mem_k, mem_v, out_q, out_
             2: [lambda: quantise_w(K, 0), lambda: lay_by_gpsimd(V, 1), lambda: lay_by_scalar(V, 1)],
             4: [lambda: quantise_x(1), lambda: quantise_w(V, 1), lambda: lay_by_gpsimd(Q, 1)],
             5: [lambda: lay_by_scalar(Q, 1)],
-            6: [lambda: quantise_w(Q, 1), lambda: lay_by_gpsimd(K, 1), lambda: lay_by_scalar(K, 1)],
-            8: [lambda: quantise_w(K, 1)],
-            12: [memory_sums],
-            15: [memory_factors],
-            16: [memory_rows],
+            7: [lambda: quantise_w(Q, 1), lambda: lay_by_gpsimd(K, 1), lambda: lay_by_scalar(K, 1)],
+            10: [lambda: quantise_w(K, 1)],
+            14: [memory_sums],
+            17: [memory_factors],
+            18: [memory_rows],
         }
-        quantised = {(V, 0): 0, (Q, 0): 0, (K, 0): 2, (V, 1): 4, (Q, 1): 6, (K, 1): 8}
+        quantised = {(V, 0): 0, (Q, 0): 0, (K, 0): 2, (V, 1): 4, (Q, 1): 7, (K, 1): 10}
         batch_quantised = [0, 4]
 
         def possible(item):

@@ -158,10 +158,7 @@ def tile_attention_pa_kernel(tc, x, freqs, Wq, Wk, Wv, mem_k, mem_v, out_q, out_
             rows = x_grouped[b][:, :, j * P * PACK : (j + 1) * P * PACK]
             target = rows.bitcast(F32).rearrange("p g (r u) -> p g r u", u=2)
             source = transposed[:].rearrange("p (g u) r -> p g r u", g=PASSES)
-            if b == 0 and j >= 2:
-                nc.vector.tensor_copy(out=target, in_=source)
-            else:
-                nc.scalar.copy(out=target, in_=source)
+            nc.scalar.copy(out=target, in_=source)
 
         def quantise_x(b):
             nc.vector.quantize_mx(
@@ -358,18 +355,18 @@ def tile_attention_pa_kernel(tc, x, freqs, Wq, Wk, Wv, mem_k, mem_v, out_q, out_
         mem_shape = [MEM_GROUPS * HEADS, MEM_ROWS, FEATURES]
         mem_k_sq = keep.tile(mem_shape, F32)
         mem_k_ss = keep.tile(mem_shape[:2], F32)
-        mem_k_rsqrt = keep.tile(mem_shape[:2], F32)
+        mem_k_above = keep.tile(mem_shape[:2], F32)
         mem_k_factor = keep.tile(mem_shape[:2], F32)
         mem_k_out = keep.tile(mem_shape, F32)
         mem_v_out = keep.tile(mem_shape, F32)
 
-        def memory_sums():
-            nc.scalar.activation(out=mem_k_sq[:], in_=mem_k_raw[:], func=ACT.Square)
-            nc.vector.tensor_reduce(out=mem_k_ss[:], in_=mem_k_sq[:], axis=mybir.AxisListType.X, op=ALU.add)
-
         def memory_factors():
-            nc.scalar.activation(out=mem_k_rsqrt[:], in_=mem_k_ss[:], func=ACT.Abs_reciprocal_sqrt)
-            nc.vector.tensor_scalar_min(out=mem_k_factor[:], in0=mem_k_rsqrt[:], scalar1=1.0 / EPS)
+            for row in range(MEM_ROWS):
+                nc.scalar.activation(
+                    out=mem_k_sq[:, row, :], in_=mem_k_raw[:, row, :], func=ACT.Square, accum_out=mem_k_ss[:, row : row + 1]
+                )
+            nc.scalar.activation(out=mem_k_above[:], in_=mem_k_ss[:], func=ACT.Relu, bias=-EPS * EPS)
+            nc.scalar.activation(out=mem_k_factor[:], in_=mem_k_above[:], func=ACT.Abs_reciprocal_sqrt, bias=EPS * EPS)
 
         def memory_rows():
             nc.gpsimd.tensor_tensor(
@@ -392,15 +389,15 @@ def tile_attention_pa_kernel(tc, x, freqs, Wq, Wk, Wv, mem_k, mem_v, out_q, out_
                 transpose_x_tile(token_tile)
             for u in range(2):
                 turn_table(u)
-            lay_by_scalar(V, 0)
+            for w in (V, Q):
+                lay_by_scalar(w, 0)
             for u in range(2):
                 nc.scalar.copy(out=turned_table[:, u, :], in_=turned[u][:])
-            quantise_x(0)
+            lay_by_scalar(K, 0)
             lay_by_vector(V, 0, "by_vector")
+            quantise_x(0)
             lay_by_vector(Q, 0, "by_other")
             quantise_w(V, 0)
-            for w in (Q, K):
-                lay_by_scalar(w, 0)
             quantise_w(Q, 0)
             lay_by_gpsimd(K, 0)
 
@@ -421,8 +418,7 @@ def tile_attention_pa_kernel(tc, x, freqs, Wq, Wk, Wv, mem_k, mem_v, out_q, out_
             5: [lambda: lay_by_scalar(Q, 1)],
             7: [lambda: quantise_w(Q, 1), lambda: lay_by_gpsimd(K, 1), lambda: lay_by_scalar(K, 1)],
             10: [lambda: quantise_w(K, 1)],
-            14: [memory_sums],
-            17: [memory_factors],
+            14: [memory_factors],
             18: [memory_rows],
         }
         quantised = {(V, 0): 0, (Q, 0): 0, (K, 0): 2, (V, 1): 4, (Q, 1): 7, (K, 1): 10}

from contextlib import ExitStack

import concourse.mybir as mybir
from concourse.masks import make_identity

F32 = mybir.dt.float32
BF16 = mybir.dt.bfloat16
U32 = mybir.dt.uint32
U8 = mybir.dt.uint8
FP8X4 = mybir.dt.float8_e4m3fn_x4
ACT = mybir.ActivationFunctionType
ALU = mybir.AluOpType

BATCH, POSITIONS, DIM, HEADS, FEATURES, MEM_SLOTS = 2, 512, 1024, 16, 64, 16
HALF = FEATURES // 2
EPS = 1e-12

P = 128
PACK = 4
K_PASS = P * PACK
PASSES = DIM // K_PASS
Q, K, V = 0, 1, 2
LATE_V = (2, 4, 7, 10, 12, 15)
EARLY_V = 10
TILES_PER_BATCH = POSITIONS // P
TOKEN_TILES = BATCH * TILES_PER_BATCH
TILES_PER_STORE = 2
BANK_COLUMNS = 512
BANK_HEADS = BANK_COLUMNS // FEATURES
PARTS = HEADS // BANK_HEADS
UNITS = PARTS * TOKEN_TILES
PAIR = 2 * FEATURES
PAIRS_PER_PART = BANK_COLUMNS // PAIR
PAIRS_PER_STORE = 1
MEM_GROUPS = 4
MEM_ROWS = MEM_SLOTS // MEM_GROUPS
GPSIMD_V = ()
WORDS_PER_PASS = K_PASS // 2

FLOPS = 2 * BATCH * POSITIONS * DIM * 3 * HEADS * FEATURES


def tile_attention_pa_kernel(tc, x, freqs, Wq, Wk, Wv, mem_k, mem_v, out_q, out_k, out_v):
    nc = tc.nc
    weights = [Wq, Wk, Wv]
    outputs = [out_q, out_k, out_v]
    first_position = [0, MEM_SLOTS, MEM_SLOTS]

    with ExitStack() as ctx:
        keep = ctx.enter_context(tc.tile_pool(name="keep", bufs=1))
        stage = ctx.enter_context(tc.tile_pool(name="stage", bufs=2))
        norms = ctx.enter_context(tc.tile_pool(name="norms", bufs=8))
        rotated = ctx.enter_context(tc.tile_pool(name="rotated", bufs=8))
        results = ctx.enter_context(tc.tile_pool(name="results", bufs=3))
        psum_aux = ctx.enter_context(tc.psum_pool(name="psum_aux", bufs=3))
        psum_acc = ctx.enter_context(tc.psum_pool(name="psum_acc", bufs=5))

        angles = keep.tile([P, TILES_PER_BATCH, 2, HALF], BF16)
        nc.scalar.dma_start(out=angles[:], in_=freqs.rearrange("(p j) (a c) -> p j a c", j=TILES_PER_BATCH, a=2))

        x_raw = [keep.tile([P, DIM], BF16, name="x_raw%d" % t) for t in range(TOKEN_TILES)]
        w_raw = [
            [keep.tile([P, PASSES, PACK, BANK_COLUMNS], BF16, name="w_raw%d_%d" % (w, part)) for part in range(PARTS)]
            for w in range(len(weights))
        ]

        def load_x(token_tile):
            b, j = divmod(token_tile, TILES_PER_BATCH)
            nc.sync.dma_start(
                out=x_raw[token_tile][:], in_=x[b].rearrange("(p j) k -> p j k", j=TILES_PER_BATCH)[:, j, :]
            )

        def load_w(w, part):
            for g in range(PASSES):
                nc.sync.dma_start(
                    out=w_raw[w][part][:, g],
                    in_=weights[w][
                        g * K_PASS : (g + 1) * K_PASS, part * BANK_COLUMNS : (part + 1) * BANK_COLUMNS
                    ].rearrange("(p t) n -> p t n", t=PACK),
                )

        for token_tile in range(TILES_PER_BATCH):
            load_x(token_tile)
        for w in (V, Q, K):
            load_w(w, 0)
        for token_tile in range(TILES_PER_BATCH, TOKEN_TILES):
            load_x(token_tile)
        for w in (V, Q, K):
            load_w(w, 1)
        mem_k_raw = keep.tile([MEM_GROUPS * HEADS, MEM_ROWS, FEATURES], BF16)
        mem_v_raw = keep.tile([MEM_GROUPS * HEADS, MEM_ROWS, FEATURES], BF16)
        for group in range(MEM_GROUPS):
            heads = slice(group * HEADS, (group + 1) * HEADS)
            slots = slice(group * MEM_ROWS, (group + 1) * MEM_ROWS)
            nc.sync.dma_start(out=mem_k_raw[heads], in_=mem_k[:, slots, :])
            nc.sync.dma_start(out=mem_v_raw[heads], in_=mem_v[:, slots, :])

        ctx.enter_context(tc.manual_schedule(engines={mybir.EngineType.DVE, mybir.EngineType.Pool}))

        identity = keep.tile([P, P], F32)
        make_identity(nc, identity[:])
        moves = keep.tile([P, 2, 2, FEATURES], F32)
        for u in range(2):
            straight = slice(u * FEATURES, (u + 1) * FEATURES)
            nc.vector.tensor_copy(out=moves[:, u, u, :], in_=identity[:, straight])
            for half in range(2):
                source = (1 - u) * FEATURES + (1 - half) * HALF
                nc.vector.tensor_copy(
                    out=moves[:, u, 1 - u, half * HALF : (half + 1) * HALF], in_=identity[:, source : source + HALF]
                )

        half_sin = keep.tile([P, TILES_PER_BATCH, 2, HALF], F32)
        half_sin_sq = keep.tile([P, TILES_PER_BATCH, 2, HALF], F32)
        table = keep.tile([P, TILES_PER_BATCH, 2, 2, HALF], F32)
        blocks = keep.tile([P, TILES_PER_BATCH, 6, HALF], F32)
        inverse_of_one = keep.tile([P, 1], F32)

        def build_tables():
            nc.scalar.activation(out=half_sin[:], in_=angles[:], func=ACT.Sin, scale=0.5)
            for target in (blocks[:, :, 2, :], table[:, :, 1, 0, :]):
                nc.scalar.activation(out=target, in_=angles[:, :, 1, :], func=ACT.Sin)
            for target in (blocks[:, :, 3, :], table[:, :, 0, 1, :]):
                nc.scalar.activation(out=target, in_=angles[:, :, 0, :], func=ACT.Sin, scale=-1.0)
            nc.scalar.activation(
                out=inverse_of_one[:], in_=table[:, 0, 0, 1, 0:1], func=ACT.Abs_reciprocal_sqrt, scale=0.0, bias=1.0
            )
            nc.vector.tensor_tensor(out=half_sin_sq[:], in0=half_sin[:], in1=half_sin[:], op=ALU.mult)
            for first in (0, 4):
                nc.vector.tensor_scalar(
                    out=blocks[:, :, first : first + 2, :], in0=half_sin_sq[:], scalar1=-2.0, scalar2=1.0, op0=ALU.mult, op1=ALU.add
                )
            for a in range(2):
                nc.gpsimd.tensor_scalar(
                    out=table[:, :, a, a, :], in0=half_sin_sq[:, :, a, :], scalar1=-2.0, scalar2=1.0, op0=ALU.mult, op1=ALU.add
                )

        turned_table = keep.tile([P, 2, POSITIONS], F32)

        x_codes = keep.tile([P, BATCH, PASSES * POSITIONS], U32, align_bytes=64)
        x_scales = keep.tile([P, BATCH, PASSES * POSITIONS], U8, align_bytes=64)
        w_codes = keep.tile([P, len(weights) * PARTS, PASSES * BANK_COLUMNS], U32, align_bytes=64)
        w_scales = keep.tile([P, len(weights) * PARTS, PASSES * BANK_COLUMNS], U8, align_bytes=64)
        x_grouped = [None] * BATCH
        w_grouped = [[None, None] for r in range(len(weights) * PARTS)]

        def transpose_x_tile(token_tile):
            b, j = divmod(token_tile, TILES_PER_BATCH)
            if j == 0:
                x_grouped[b] = keep.tile([P, PASSES, POSITIONS * PACK], BF16, name="x_grouped%d" % b, align_bytes=64)
            words = x_raw[token_tile][:].bitcast(F32)
            transposed = psum_acc.tile([P, PASSES * 2, P], F32, name="acc")
            for g in range(PASSES):
                for u in range(2):
                    first_word = g * WORDS_PER_PASS + u
                    nc.tensor.transpose(
                        transposed[:, 2 * g + u, :], words[:, first_word : first_word + WORDS_PER_PASS - 1 : 2], identity[:]
                    )
            rows = x_grouped[b][:, :, j * P * PACK : (j + 1) * P * PACK]
            target = rows.bitcast(F32).rearrange("p g (r u) -> p g r u", u=2)
            source = transposed[:].rearrange("p (g u) r -> p g r u", g=PASSES)
            nc.scalar.copy(out=target, in_=source)

        def quantise_x(b):
            nc.vector.quantize_mx(
                out=x_codes[:, b, :].bitcast(FP8X4),
                scales=x_scales[:, b, :],
                in_=x_grouped[b][:].rearrange("p g n -> p (g n)"),
            )

        turned = [None, None]

        def turn_table(u):
            turned[u] = psum_acc.tile([P, POSITIONS], F32, name="acc")
            for j in range(TILES_PER_BATCH):
                nc.tensor.transpose(
                    turned[u][:, j * P : (j + 1) * P],
                    blocks[:, j, 2 * u : 2 * u + 4, :].rearrange("p b c -> p (b c)"),
                    identity[:],
                )

        def lay_by_scalar(w, part):
            grouped = stage.tile([P, BANK_COLUMNS, PACK], BF16, name="by_scalar", align_bytes=64)
            w_grouped[w * PARTS + part][0] = grouped
            nc.scalar.copy(
                out=grouped[:].rearrange("p (c i) t -> p c t i", i=4),
                in_=w_raw[w][part][:, 0].rearrange("p t (c i) -> p c t i", i=4),
            )

        def lay_by_vector(w, part, name):
            grouped = keep.tile([P, BANK_COLUMNS, PACK], BF16, name=name, align_bytes=64)
            w_grouped[w * PARTS + part][1] = grouped
            nc.vector.tensor_copy(
                out=grouped[:].rearrange("p (c i) t -> p c t i", i=4),
                in_=w_raw[w][part][:, 1].rearrange("p t (c i) -> p c t i", i=4),
            )

        def lay_by_gpsimd(w, part):
            grouped = keep.tile([P, BANK_COLUMNS, PACK], BF16, name="by_other", align_bytes=64)
            w_grouped[w * PARTS + part][1] = grouped
            nc.gpsimd.tensor_scalar(
                out=grouped[:],
                in0=w_raw[w][part][:, 1].rearrange("p t n -> p n t"),
                scalar1=1.0,
                scalar2=0.0,
                op0=ALU.mult,
                op1=ALU.add,
            )

        def quantise_w(w, part):
            r = w * PARTS + part
            for g in range(PASSES):
                columns = slice(g * BANK_COLUMNS, (g + 1) * BANK_COLUMNS)
                nc.vector.quantize_mx(
                    out=w_codes[:, r, columns].bitcast(FP8X4),
                    scales=w_scales[:, r, columns],
                    in_=w_grouped[r][g][:].rearrange("p n t -> p (n t)"),
                )

        state = {}
        open_result = [None] * len(weights)

        def matmuls(item):
            w, unit = item
            part, place_in_part = divmod(unit, TOKEN_TILES)
            b, place = divmod(place_in_part, TILES_PER_BATCH)
            r = w * PARTS + part
            acc = psum_acc.tile([P, BANK_COLUMNS], F32, name="acc")
            state[item] = {"acc": acc}
            for g in range(PASSES):
                if w == V:
                    tokens = slice(g * POSITIONS, (g + 1) * POSITIONS)
                    columns = slice(g * BANK_COLUMNS + place * PAIR, g * BANK_COLUMNS + (place + 1) * PAIR)
                    still, moving = (w_codes[:, r, columns], w_scales[:, r, columns]), (x_codes[:, b, tokens], x_scales[:, b, tokens])
                else:
                    tokens = slice(g * POSITIONS + place * P, g * POSITIONS + (place + 1) * P)
                    columns = slice(g * BANK_COLUMNS, (g + 1) * BANK_COLUMNS)
                    still, moving = (x_codes[:, b, tokens], x_scales[:, b, tokens]), (w_codes[:, r, columns], w_scales[:, r, columns])
                nc.tensor.matmul_mx(
                    out=acc[:],
                    lhsT=still[0].bitcast(FP8X4),
                    lhsT_scale=still[1],
                    rhs=moving[0].bitcast(FP8X4),
                    rhs_scale=moving[1],
                    start=(g == 0),
                    stop=(g == PASSES - 1),
                )

        def sum_squares(item, heads):
            acc = state[item]["acc"]
            if heads[0] == 0:
                state[item]["sum_sq"] = norms.tile([P, BANK_HEADS], F32, name="sum_sq")
                state[item]["squares"] = stage.tile([P, BANK_HEADS, FEATURES], F32, name="squares")
            for h in heads:
                nc.scalar.activation(
                    out=state[item]["squares"][:, h, :],
                    in_=acc[:, h * FEATURES : (h + 1) * FEATURES],
                    func=ACT.Square,
                    accum_out=state[item]["sum_sq"][:, h : h + 1],
                )

        def clip(item):
            above = norms.tile([P, BANK_HEADS], F32, name="above")
            state[item]["above"] = above
            nc.scalar.activation(out=above[:], in_=state[item]["sum_sq"][:], func=ACT.Relu, bias=-EPS * EPS)

        def invert(item):
            factor = norms.tile([P, BANK_HEADS], F32, name="factor")
            state[item]["factor"] = factor
            nc.scalar.activation(out=factor[:], in_=state[item]["above"][:], func=ACT.Abs_reciprocal_sqrt, bias=EPS * EPS)

        def multiply(item):
            w, unit = item
            acc = state[item]["acc"]
            products = rotated.tile([P, 2 * BANK_COLUMNS], F32, name="products")
            state[item]["products"] = products
            if w == V:
                shape = [P, 2, POSITIONS]
                engine, values = nc.vector, acc
                if unit in GPSIMD_V:
                    engine, values = nc.gpsimd, stage.tile([P, POSITIONS], F32, name="values")
                    nc.scalar.copy(out=values[:], in_=acc[:])
                engine.tensor_tensor(
                    out=products[:].rearrange("p (u n) -> p u n", u=2),
                    in0=values[:].unsqueeze(1).to_broadcast(shape),
                    in1=turned_table[:],
                    op=ALU.mult,
                )
                return
            by_head = products[:].rearrange("p (h o d) -> p h o d", h=BANK_HEADS, o=2)
            spread = acc[:].rearrange("p (h d) -> p h d", d=FEATURES).unsqueeze(2).to_broadcast([P, BANK_HEADS, 2, FEATURES])
            for h in range(BANK_HEADS):
                nc.vector.scalar_tensor_tensor(
                    out=by_head[:, h],
                    in0=spread[:, h],
                    scalar=state[item]["factor"][:, h : h + 1],
                    in1=table[:, unit % TILES_PER_BATCH].rearrange("p o a c -> p o (a c)"),
                    op0=ALU.mult,
                    op1=ALU.mult,
                )

        def add(item):
            w, unit = item
            place = unit % TILES_PER_STORE
            if place == 0:
                open_result[w] = results.tile([P, BANK_HEADS, TILES_PER_STORE, FEATURES], F32, name="result%d" % w)
            by_half = state[item]["products"][:].rearrange("p (h o a c) -> p h o a c", h=BANK_HEADS, o=2, a=2)
            nc.gpsimd.tensor_tensor(
                out=open_result[w][:, :, place, :].rearrange("p h (o c) -> p h o c", o=2),
                in0=by_half[:, :, :, 0, :],
                in1=by_half[:, :, :, 1, :],
                op=ALU.add,
            )
            if place == TILES_PER_STORE - 1:
                part, place_in_part = divmod(unit, TOKEN_TILES)
                b, j = divmod(place_in_part, TILES_PER_BATCH)
                heads = slice(part * BANK_HEADS, (part + 1) * BANK_HEADS)
                positions = slice(first_position[w], first_position[w] + POSITIONS)
                by_tile = outputs[w][b, heads, positions, :].rearrange("h (p j) d -> p h j d", j=TILES_PER_BATCH)
                nc.sync.dma_start(out=by_tile[:, :, j - place : j + 1, :], in_=open_result[w][:])

        def turn_back(item):
            products = state[item]["products"][:].rearrange("p (u n) -> p u n", u=2)
            total = psum_aux.tile([P, TILES_PER_BATCH, PAIR], F32, name="aux")
            state[item]["total"] = total
            for j in range(TILES_PER_BATCH):
                for u in range(2):
                    nc.tensor.matmul(
                        out=total[:, j, :],
                        lhsT=products[:, u, j * P : (j + 1) * P],
                        rhs=moves[:, u].rearrange("p h d -> p (h d)"),
                        is_transpose=True,
                        start=(u == 0),
                        stop=(u == 1),
                    )

        def copy_back(item):
            w, unit = item
            part, place_in_part = divmod(unit, TOKEN_TILES)
            b, pair = divmod(place_in_part, PAIRS_PER_PART)
            place = pair % PAIRS_PER_STORE
            if place == 0:
                open_result[w] = results.tile([P, 2 * PAIRS_PER_STORE, TILES_PER_BATCH, FEATURES], F32, name="result2")
            nc.scalar.copy(
                out=open_result[w][:, 2 * place : 2 * place + 2].rearrange("p h j d -> p j h d"),
                in_=state[item]["total"][:].rearrange("p j (h d) -> p j h d", h=2),
            )
            if place == PAIRS_PER_STORE - 1:
                first_head = part * BANK_HEADS + 2 * (pair - place)
                rows_of_heads = out_v[b, first_head : first_head + 2 * PAIRS_PER_STORE, MEM_SLOTS : MEM_SLOTS + POSITIONS, :]
                nc.sync.dma_start(
                    out=rows_of_heads.rearrange("h (p j) d -> p h (j d)", j=TILES_PER_BATCH),
                    in_=open_result[w][:].rearrange("p h j d -> p h (j d)"),
                )

        mem_shape = [MEM_GROUPS * HEADS, MEM_ROWS, FEATURES]
        mem_k_sq = keep.tile(mem_shape, F32)
        mem_k_ss = keep.tile(mem_shape[:2], F32)
        mem_k_above = keep.tile(mem_shape[:2], F32)
        mem_k_factor = keep.tile(mem_shape[:2], F32)
        mem_k_out = keep.tile(mem_shape, F32)
        mem_v_out = keep.tile(mem_shape, F32)

        def memory_factors():
            for row in range(MEM_ROWS):
                nc.scalar.activation(
                    out=mem_k_sq[:, row, :], in_=mem_k_raw[:, row, :], func=ACT.Square, accum_out=mem_k_ss[:, row : row + 1]
                )
            nc.scalar.activation(out=mem_k_above[:], in_=mem_k_ss[:], func=ACT.Relu, bias=-EPS * EPS)
            nc.scalar.activation(out=mem_k_factor[:], in_=mem_k_above[:], func=ACT.Abs_reciprocal_sqrt, bias=EPS * EPS)

        def memory_rows():
            nc.gpsimd.tensor_tensor(
                out=mem_k_out[:], in0=mem_k_raw[:], in1=mem_k_factor[:].unsqueeze(2).to_broadcast(mem_shape), op=ALU.mult
            )
            nc.gpsimd.tensor_scalar(
                out=mem_v_out[:], in0=mem_v_raw[:], scalar1=1.0, scalar2=0.0, op0=ALU.mult, op1=ALU.add
            )
            for b in range(BATCH):
                for group in range(MEM_GROUPS):
                    heads = slice(group * HEADS, (group + 1) * HEADS)
                    slots = slice(group * MEM_ROWS, (group + 1) * MEM_ROWS)
                    nc.sync.dma_start(out=out_k[b, :, slots, :], in_=mem_k_out[heads])
                    nc.sync.dma_start(out=out_v[b, :, slots, :], in_=mem_v_out[heads])

        pinned = {mybir.EngineType.DVE, mybir.EngineType.Pool, mybir.EngineType.Activation}
        with tc.manual_schedule(engines=pinned):
            build_tables()
            for token_tile in range(TILES_PER_BATCH):
                transpose_x_tile(token_tile)
            for u in range(2):
                turn_table(u)
            for w in (V, Q):
                lay_by_scalar(w, 0)
            for u in range(2):
                nc.scalar.copy(out=turned_table[:, u, :], in_=turned[u][:])
            lay_by_scalar(K, 0)
            lay_by_vector(V, 0, "by_vector")
            quantise_x(0)
            lay_by_vector(Q, 0, "by_other")
            quantise_w(V, 0)
            quantise_w(Q, 0)
            lay_by_gpsimd(K, 0)

        items = [(V, unit) for unit in range(EARLY_V)]
        for unit in range(UNITS):
            items += [(Q, unit), (K, unit)]
            if unit in LATE_V:
                items.append((V, EARLY_V + LATE_V.index(unit)))

        def second_batch():
            for token_tile in range(TILES_PER_BATCH, TOKEN_TILES):
                transpose_x_tile(token_tile)

        before = {
            1: [second_batch],
            2: [lambda: quantise_w(K, 0), lambda: lay_by_gpsimd(V, 1), lambda: lay_by_scalar(V, 1)],
            4: [lambda: quantise_x(1), lambda: quantise_w(V, 1), lambda: lay_by_gpsimd(Q, 1)],
            5: [lambda: lay_by_scalar(Q, 1)],
            7: [lambda: quantise_w(Q, 1), lambda: lay_by_gpsimd(K, 1), lambda: lay_by_scalar(K, 1)],
            10: [lambda: quantise_w(K, 1)],
            14: [memory_factors],
            18: [memory_rows],
        }
        quantised = {(V, 0): 0, (Q, 0): 0, (K, 0): 2, (V, 1): 4, (Q, 1): 7, (K, 1): 10}
        batch_quantised = [0, 4]

        def possible(item):
            part, place_in_part = divmod(item[1], TOKEN_TILES)
            return max(quantised[item[0], part], batch_quantised[place_in_part // TILES_PER_BATCH])

        last = len(items) - 1
        normed = [index for index in range(len(items)) if items[index][0] != V]
        issued, summed, inverted = 0, 0, 0
        for tick in range(len(items) + 2):
            for step in before.get(tick, []):
                step()
            while issued <= min(last, tick + (5 if tick else 1)) and possible(items[issued]) <= tick:
                matmuls(items[issued])
                issued += 1
            while summed < len(normed) and normed[summed] <= tick + 3 and normed[summed] < issued:
                sum_squares(items[normed[summed]], range(0, BANK_HEADS // 2))
                if inverted < summed:
                    clip(items[normed[inverted]])
                sum_squares(items[normed[summed]], range(BANK_HEADS // 2, BANK_HEADS))
                if inverted < summed:
                    invert(items[normed[inverted]])
                    inverted += 1
                summed += 1
            if inverted < summed and normed[inverted] <= tick + 1:
                clip(items[normed[inverted]])
                invert(items[normed[inverted]])
                inverted += 1
            if tick >= 2 and items[tick - 2][0] == V:
                copy_back(items[tick - 2])
            if tick <= last:
                multiply(items[tick])
                if items[tick][0] != V:
                    add(items[tick])
            if 1 <= tick <= last + 1 and items[tick - 1][0] == V:
                turn_back(items[tick - 1])
